import numpy as np
import ml_dtypes


def mxq(x, axis, fmt="e4m3"):
    dtype, down = {"e4m3": (ml_dtypes.float8_e4m3fn, 7), "e5m2": (ml_dtypes.float8_e5m2, 14)}[fmt]
    v = np.moveaxis(np.asarray(x, np.float32).astype(ml_dtypes.bfloat16).astype(np.float64), axis, -1)
    blocks = v.reshape(v.shape[:-1] + (-1, 32))
    amax = np.abs(blocks).max(-1, keepdims=True)
    byte = np.maximum(np.where(amax > 0, np.frexp(amax)[1] - 1 + 127, 0) - down, 1)
    scale = np.exp2(byte - 127.0)
    codes = (blocks / scale).astype(np.float32).astype(dtype).astype(np.float64)
    return np.moveaxis((codes * scale).reshape(v.shape), -1, axis)


WIDE = False


def mx_kscale(k):
    if not WIDE:
        return np.ones(k)
    levels = np.array([10, -10, 5, -5, 0])
    if k % 512:
        return np.exp2(np.random.permutation(np.resize(levels, k // 32))).repeat(32)
    a = np.empty((k // 512, 16))
    for p in range(k // 512):
        a[p, :8] = np.random.permutation(np.resize(levels, 8))
        for g in range(8):
            far = levels[np.abs(levels - a[p, g]) >= 10]
            a[p, g + 8] = far[np.random.randint(len(far))]
    return np.exp2(a.ravel()).repeat(32)


BF16 = ml_dtypes.bfloat16


def bf(x):
    return np.asarray(x, np.float32).astype(BF16)


def f64(x):
    return np.asarray(x).astype(np.float64)


B, S, HID, H, HK, D = 2, 256, 2048, 16, 4, 128
EPS = 1e-6
PRE = 0.004


def rmsnorm(v, w):
    var = np.mean(v * v, axis=-1, keepdims=True)
    return w * (v * (1.0 / np.sqrt(var + EPS)))


def rope(v, cos, sin):
    c = cos[:, :, None, :]
    sn = sin[:, :, None, :]
    v1, v2 = np.split(v, 2, axis=-1)
    rot = np.concatenate([-v2, v1], axis=-1)
    return v * c + rot * sn


def draw0():
    s = mx_kscale(HID)
    return {
        "hidden_states": bf(np.random.standard_normal((B, S, HID)) * s),
        "cos": bf(np.cos(np.random.standard_normal((B, S, D)))),
        "sin": bf(np.sin(np.random.standard_normal((B, S, D)))),
        "Wq_query": bf(np.random.standard_normal((H * D, HID)) * PRE / np.sqrt(HID) / s),
        "Wk": bf(np.random.standard_normal((HK * D, HID)) * PRE / np.sqrt(HID) / s),
        "q_norm_w": bf(1.0 + 0.1 * np.random.standard_normal(D)),
        "k_norm_w": bf(1.0 + 0.1 * np.random.standard_normal(D)),
    }


def core(hidden_states, cos, sin, Wq_query, Wk, q_norm_w, k_norm_w):
    xq = mxq(f64(hidden_states), 2, "e4m3")
    q = (xq @ mxq(f64(Wq_query), 1, "e4m3").T).reshape(B, S, H, D)
    k = (xq @ mxq(f64(Wk), 1, "e4m3").T).reshape(B, S, HK, D)
    q = rmsnorm(q, f64(q_norm_w))
    k = rmsnorm(k, f64(k_norm_w))
    q = rope(q, f64(cos), f64(sin))
    k = rope(k, f64(cos), f64(sin))
    return q, k


def e4m3fn_bytes(y):
    return np.clip(np.asarray(y, np.float64), -448.0, 448.0).astype(np.float32).astype(ml_dtypes.float8_e4m3fn).view(np.uint8)


def e4m3fn_values(b):
    return np.asarray(b, np.uint8).view(ml_dtypes.float8_e4m3fn).astype(np.float64)


def setup_inputs():
    d = draw0()
    x0 = np.asarray(d['Wq_query']).astype(np.float64)
    s = (np.max(np.abs(x0), axis=(0,), keepdims=True) / 448.0).astype(np.float32)
    out = {}
    for k, v in d.items():
        if k == 'Wq_query':
            out['Wq_query_bytes'] = e4m3fn_bytes(x0 / s.astype(np.float64))
            out['Wq_query_scale'] = s
        else:
            out[k] = v
    return out


def reference(hidden_states, cos, sin, Wq_query_bytes, Wq_query_scale, Wk, q_norm_w, k_norm_w):
    return core(hidden_states, cos, sin, e4m3fn_values(Wq_query_bytes) * Wq_query_scale.astype(np.float64), Wk, q_norm_w, k_norm_w)

@@ -1,0 +1,469 @@
+from contextlib import ExitStack
+
+import concourse.mybir as mybir
+from concourse.masks import make_identity
+
+F32 = mybir.dt.float32
+BF16 = mybir.dt.bfloat16
+U32 = mybir.dt.uint32
+U8 = mybir.dt.uint8
+FP8 = mybir.dt.float8_e4m3fn
+FP8X4 = mybir.dt.float8_e4m3fn_x4
+ALU = mybir.AluOpType
+ACT = mybir.ActivationFunctionType
+
+P = 128
+TOK = 512
+HID = 2048
+D = 128
+HALF = 64
+PASSES = 4
+NT = 4
+GROUP = 512
+HG = 4
+NQ = 4
+EPS = 1e-6
+
+FLOPS = 2 * TOK * HID * (2048 + 512)
+
+
+def tile_qwen3nextattentionforengine_pa_kernel(
+    tc, hidden_states, cos, sin, Wq_query_bytes, Wq_query_scale, Wk, q_norm_w, k_norm_w, out_0, out_1
+):
+    nc = tc.nc
+    x_hbm = hidden_states.flatten_outer_dims()
+    cos_hbm = cos.flatten_outer_dims()
+    sin_hbm = sin.flatten_outer_dims()
+    q_hbm = out_0.rearrange("b s h d -> (b s) (h d)")
+    k_hbm = out_1.rearrange("b s h d -> (b s) (h d)")
+
+    with ExitStack() as ctx:
+        keep = ctx.enter_context(tc.tile_pool(name="keep", bufs=1))
+        raw = ctx.enter_context(tc.tile_pool(name="raw", bufs=3))
+        wide = ctx.enter_context(tc.tile_pool(name="wide", bufs=4))
+        grp = ctx.enter_context(tc.tile_pool(name="grp", bufs=2))
+        epi = ctx.enter_context(tc.tile_pool(name="epi", bufs=8))
+        small = ctx.enter_context(tc.tile_pool(name="small", bufs=12))
+        work = ctx.enter_context(tc.tile_pool(name="work", bufs=4))
+        psum_t = ctx.enter_context(tc.psum_pool(name="psum_t", bufs=4))
+        psum_a = ctx.enter_context(tc.psum_pool(name="psum_a", bufs=4))
+        ctx.enter_context(tc.manual_schedule())
+
+        cos_sb = keep.tile([P, NT, D], BF16, name="cos_sb")
+        sin_sb = keep.tile([P, NT, D], BF16, name="sin_sb")
+        scale_bc = keep.tile([P, HID], F32, name="scale_bc")
+
+        wq_bytes = []
+        x_sb = []
+        wk_sb = []
+
+        def load_scale(c0, c1):
+            nc.sync.dma_start(
+                out=scale_bc[:, c0:c1],
+                in_=Wq_query_scale[0:1, c0:c1].rearrange("o k -> (o k)").partition_broadcast(P),
+            )
+
+        def new_bytes():
+            wq_raw = raw.tile([P, HG, HID], U8, name="wq_raw")
+            wq_bytes.append(wq_raw)
+
+        def load_bytes_pass(j, g, r0, r1):
+            cols = slice(g * 512, (g + 1) * 512)
+            nc.sync.dma_start(
+                out=wq_bytes[j][:, r0:r1, cols],
+                in_=Wq_query_bytes[(HG * j + r0) * P:(HG * j + r1) * P, cols].rearrange("(r p) c -> p r c", p=P),
+            )
+
+        def load_bytes_rows(j, r):
+            rt = HG * j + r
+            nc.sync.dma_start(out=wq_bytes[j][:, r, :], in_=Wq_query_bytes[rt * P:(rt + 1) * P, :])
+
+        def load_x(t):
+            xt = keep.tile([P, HID], BF16, name="x_sb%d" % t)
+            nc.sync.dma_start(out=xt[:], in_=x_hbm[t * P:(t + 1) * P, :])
+            x_sb.append(xt)
+
+        for j in range(3):
+            new_bytes()
+        load_scale(0, 256)
+        load_bytes_pass(0, 0, 0, 2)
+        load_scale(256, 512)
+        scale_rows = []
+        for g in range(1, 4):
+            row = epi.tile([P, GROUP], F32, name="a_sb")
+            nc.vector.memset(row[:], 0.0)
+            nc.sync.dma_start(out=row[0:1, :], in_=Wq_query_scale[0:1, g * 512:(g + 1) * 512])
+            scale_rows.append(row)
+        load_bytes_pass(0, 0, 2, 4)
+        load_bytes_pass(1, 0, 0, 4)
+        for g in range(1, 4):
+            load_bytes_pass(0, g, 0, 4)
+            load_bytes_pass(1, g, 0, 4)
+            load_x(g - 1)
+        load_x(3)
+        nc.sync.dma_start(out=cos_sb[:], in_=cos_hbm.rearrange("(t p) d -> p t d", p=P))
+        nc.sync.dma_start(out=sin_sb[:], in_=sin_hbm.rearrange("(t p) d -> p t d", p=P))
+        w_cols = []
+        for w_hbm, nm in ((q_norm_w, "q"), (k_norm_w, "k")):
+            col = w_hbm.rearrange("(d o) -> d o", o=1)
+            w_plain = keep.tile([P, 1], BF16, name="w_plain_" + nm)
+            w_swap = keep.tile([P, 1], BF16, name="w_swap_" + nm)
+            nc.sync.dma_start(out=w_plain[:], in_=col)
+            nc.sync.dma_start(out=w_swap[0:HALF, :], in_=col[HALF:D, :])
+            nc.sync.dma_start(out=w_swap[HALF:D, :], in_=col[0:HALF, :])
+            w_cols.append((w_plain, w_swap))
+        for r in range(4):
+            load_bytes_rows(2, r)
+        for t in range(4):
+            wt = keep.tile([P, HID], BF16, name="wk_sb%d" % t)
+            nc.sync.dma_start(out=wt[:], in_=Wk[t * P:(t + 1) * P, :])
+            wk_sb.append(wt)
+
+        ident = keep.tile([P, P], F32, name="ident")
+        make_identity(nc, ident[:])
+        ones = keep.tile([P, P], F32, name="ones")
+        nc.vector.memset(ones[:], 1.0)
+
+        def spread_scale(g):
+            spread = psum_t.tile([P, GROUP], F32, name="tp")
+            nc.tensor.matmul(out=spread[:], lhsT=ones[:], rhs=scale_rows[g - 1][:], start=True, stop=True)
+            nc.scalar.copy(out=scale_bc[:, g * 512:(g + 1) * 512], in_=spread[:])
+        one = keep.tile([P, 1], F32, name="one")
+        nc.gpsimd.memset(one[:], 1.0)
+        warm = keep.tile([P, 1], F32, name="warm")
+        nc.scalar.activation(out=warm[:], in_=one[:], func=ACT.Abs_reciprocal_sqrt)
+
+        ident_bf = keep.tile([P, P], BF16, name="ident_bf")
+        make_identity(nc, ident_bf[:])
+
+        tabs = []
+        for nm in ("q", "k"):
+            tab = keep.tile([P, NT, 2, D], F32, name="tab_" + nm)
+            tabs.append(tab)
+        factors = keep.tile([P, 4], F32, name="factors")
+        turned = {}
+
+        def tables_first_turn():
+            for i in range(2):
+                w_plain, w_swap = w_cols[i]
+                nc.scalar.copy(out=factors[:, 2 * i:2 * i + 1], in_=w_plain[:])
+                nc.scalar.activation(
+                    out=factors[0:HALF, 2 * i + 1:2 * i + 2], in_=w_swap[0:HALF, :], func=ACT.Copy, scale=-1.0
+                )
+                nc.scalar.copy(out=factors[HALF:D, 2 * i + 1:2 * i + 2], in_=w_swap[HALF:D, :])
+            for jj, src in enumerate((cos_sb, sin_sb)):
+                tp = psum_t.tile([P, NT, P], BF16, name="tp")
+                for t in range(NT):
+                    nc.tensor.transpose(tp[:, t, :], src[:, t, :], ident_bf[:])
+                for i in range(2):
+                    tab_t = work.tile([P, NT, P], F32, name="tab_t")
+                    nc.scalar.activation(
+                        out=tab_t[:], in_=tp[:], func=ACT.Copy, scale=factors[:, 2 * i + jj:2 * i + jj + 1]
+                    )
+                    turned[(i, jj)] = tab_t
+
+        def tables_second_turn():
+            for i in range(2):
+                for jj in range(2):
+                    tp = psum_t.tile([P, NT, P], F32, name="tp")
+                    for t in range(NT):
+                        nc.tensor.transpose(tp[:, t, :], turned[(i, jj)][:, t, :], ident[:])
+                    nc.scalar.copy(out=tabs[i][:, :, jj, :], in_=tp[:])
+
+        KG = NQ
+
+        def turn(src, grouped, slot):
+            words = src[:].bitcast(F32)
+            gw = grouped[:].bitcast(F32)
+            for g0 in (0, 2):
+                tp = psum_t.tile([P, 2, 2, P], F32, name="tp")
+                for gg in range(2):
+                    g = g0 + gg
+                    for u in range(2):
+                        nc.tensor.transpose(tp[:, gg, u, :], words[:, 256 * g + u:256 * (g + 1):2], ident[:])
+                nc.scalar.copy(
+                    out=gw[:, g0:g0 + 2, slot * P:(slot + 1) * P, :],
+                    in_=tp[:].rearrange("p g u r -> p g r u"),
+                )
+
+        def turn_pass(src, grouped, g):
+            words = src[:].bitcast(F32)
+            gw = grouped[:].bitcast(F32)
+            for r0 in (0, 2):
+                tp = psum_t.tile([P, 2, 2, P], F32, name="tp")
+                for rr in range(2):
+                    r = r0 + rr
+                    for u in range(2):
+                        nc.tensor.transpose(tp[:, rr, u, :], words[:, 256 * r + u:256 * (r + 1):2], ident[:])
+                nc.scalar.copy(
+                    out=gw[:, g, r0 * P:(r0 + 2) * P, :].rearrange("p (s r) u -> p s r u", s=2),
+                    in_=tp[:].rearrange("p s u r -> p s r u"),
+                )
+
+        def quantize(grouped, codes, scales):
+            for g in (0, 2):
+                nc.vector.quantize_mx(
+                    out=codes[:, g:g + 2, :].rearrange("p g c -> p (g c)").bitcast(FP8X4),
+                    scales=scales[:, g:g + 2, :].rearrange("p g c -> p (g c)"),
+                    in_=grouped[:, g:g + 2, :, :].rearrange("p g c t -> p (g c t)"),
+                )
+
+        grouped_of = {}
+        codes_of = {}
+        wbf_of = {}
+        acc_of = {}
+        rstd_of = {}
+        ab_of = {}
+
+        def new_grouped(j):
+            if j == KG or j == "x":
+                xk_grouped = keep.tile([P, PASSES, GROUP, 4], BF16, name="xk_grouped", align_bytes=64)
+                grouped_of[j] = xk_grouped
+            else:
+                w_grouped = grp.tile([P, PASSES, GROUP, 4], BF16, name="w_grouped", align_bytes=64)
+                grouped_of[j] = w_grouped
+
+        def widen_piece(rt, c0, c1):
+            nc.vector.tensor_tensor(
+                out=wbf_of[rt][:, c0:c1],
+                in0=wq_bytes[rt // HG][:, rt % HG, c0:c1].bitcast(FP8),
+                in1=scale_bc[:, c0:c1],
+                op=ALU.mult,
+            )
+
+        def new_wbf(rt):
+            w_bf = wide.tile([P, HID], BF16, name="w_bf")
+            wbf_of[rt] = w_bf
+
+        def widen(j, r):
+            rt = 4 * j + r
+            new_wbf(rt)
+            widen_piece(rt, 0, HID)
+
+        def widen_pass(j, g, pieces):
+            w_bf = wide.tile([P, HID], BF16, name="w_bf")
+            for r, c0, c1 in pieces:
+                nc.vector.tensor_tensor(
+                    out=w_bf[:, r * 512 + c0:r * 512 + c1],
+                    in0=wq_bytes[j][:, r, g * 512 + c0:g * 512 + c1].bitcast(FP8),
+                    in1=scale_bc[:, g * 512 + c0:g * 512 + c1],
+                    op=ALU.mult,
+                )
+            turn_pass(w_bf, grouped_of[j], g)
+
+        whole = [(r, 0, 512) for r in range(4)]
+        first = [(0, 0, 256), (1, 0, 256), (0, 256, 512), (1, 256, 512), (2, 0, 512), (3, 0, 512)]
+
+        def turn_q(j, r):
+            if r == 0:
+                new_grouped(j)
+            turn(wbf_of[4 * j + r], grouped_of[j], r)
+
+        def quant_group(j):
+            if j == KG or j == "x":
+                codes = keep.tile([P, PASSES, GROUP], U32, name="codes_%s" % j, align_bytes=64)
+                scales = keep.tile([P, PASSES, GROUP], U8, name="scales_%s" % j, align_bytes=64)
+            else:
+                codes = grp.tile([P, PASSES, GROUP], U32, name="w_codes", align_bytes=64)
+                scales = grp.tile([P, PASSES, GROUP], U8, name="w_scales", align_bytes=64)
+            quantize(grouped_of[j], codes, scales)
+            codes_of[j] = (codes, scales)
+
+        def multiply(j, t):
+            x_codes, x_scales = codes_of["x"]
+            w_codes, w_scales = codes_of[j]
+            if j == KG:
+                acc = psum_t.tile([P, GROUP], F32, name="tp")
+            else:
+                acc = psum_a.tile([P, GROUP], F32, name="acc")
+            toks = slice(t * P, (t + 1) * P)
+            for g in range(PASSES):
+                nc.tensor.matmul_mx(
+                    out=acc[:],
+                    lhsT=x_codes[:, g, toks].bitcast(FP8X4),
+                    lhsT_scale=x_scales[:, g, toks],
+                    rhs=w_codes[:, g, :].bitcast(FP8X4),
+                    rhs_scale=w_scales[:, g, :],
+                    start=(g == 0),
+                    stop=(g == PASSES - 1),
+                )
+            acc_of[(j, t)] = acc
+
+        def squares(j, t):
+            acc = acc_of[(j, t)]
+            ss = small.tile([P, HG], F32, name="ss")
+            for h in range(HG):
+                junk = small.tile([P, D], BF16, name="junk")
+                nc.scalar.activation(
+                    out=junk[:], in_=acc[:, h * D:(h + 1) * D], func=ACT.Square, accum_out=ss[:, h:h + 1]
+                )
+            rstd = small.tile([P, HG], F32, name="rstd")
+            nc.scalar.activation(out=rstd[:], in_=ss[:], func=ACT.Abs_reciprocal_sqrt, scale=1.0 / D, bias=EPS)
+            rstd_of[(j, t)] = rstd
+
+        def products(j, t):
+            acc = acc_of[(j, t)]
+            tab = tabs[1] if j == KG else tabs[0]
+            a_sb = epi.tile([P, GROUP], F32, name="a_sb")
+            b_sb = epi.tile([P, GROUP], F32, name="b_sb", bufs=6)
+            nc.vector.tensor_tensor(
+                out=a_sb[:].rearrange("p (h d) -> p h d", d=D),
+                in0=tab[:, t, 0, :].unsqueeze(1).to_broadcast([P, HG, D]),
+                in1=acc[:].rearrange("p (h d) -> p h d", d=D),
+                op=ALU.mult,
+            )
+            nc.vector.tensor_tensor(
+                out=b_sb[:].rearrange("p (h two d) -> p h two d", two=2, d=HALF),
+                in0=tab[:, t, 1, :].rearrange("p (two d) -> p two d", two=2).unsqueeze(1).to_broadcast([P, HG, 2, HALF]),
+                in1=acc[:].rearrange("p (h two d) -> p h two d", two=2, d=HALF)[:, :, ::-1, :],
+                op=ALU.mult,
+            )
+            ab_of[(j, t)] = (a_sb, b_sb)
+
+        def add_on(engine, j, t):
+            a_sb, b_sb = ab_of[(j, t)]
+            engine.tensor_tensor(out=a_sb[:], in0=a_sb[:], in1=b_sb[:], op=ALU.add)
+
+        def scale_store(j, t):
+            a_sb, b_sb = ab_of[(j, t)]
+            rstd = rstd_of[(j, t)]
+            o_sb = epi.tile([P, GROUP], F32, name="o_sb", bufs=8)
+            for h in range(HG):
+                hs = slice(h * D, (h + 1) * D)
+                nc.scalar.activation(out=o_sb[:, hs], in_=a_sb[:, hs], func=ACT.Copy, scale=rstd[:, h:h + 1])
+            rows = slice(t * P, (t + 1) * P)
+            if j == KG:
+                nc.sync.dma_start(out=k_hbm[rows, :], in_=o_sb[:])
+            else:
+                nc.sync.dma_start(out=q_hbm[rows, j * GROUP:(j + 1) * GROUP], in_=o_sb[:])
+
+        def scale_store_shared(j, t):
+            a_sb, b_sb = ab_of[(j, t)]
+            rstd = rstd_of[(j, t)]
+            o_v = epi.tile([P, GROUP // 2], F32, name="o_v", bufs=1)
+            o_s = epi.tile([P, GROUP // 2], F32, name="o_s", bufs=1)
+            nc.vector.tensor_tensor(
+                out=o_v[:].rearrange("p (h d) -> p h d", d=D),
+                in0=a_sb[:, 0:2 * D].rearrange("p (h d) -> p h d", d=D),
+                in1=rstd[:, 0:2].unsqueeze(2).to_broadcast([P, 2, D]),
+                op=ALU.mult,
+            )
+            for h in (2, 3):
+                nc.scalar.activation(
+                    out=o_s[:, (h - 2) * D:(h - 1) * D], in_=a_sb[:, h * D:(h + 1) * D], func=ACT.Copy, scale=rstd[:, h:h + 1]
+                )
+            rows = slice(t * P, (t + 1) * P)
+            nc.sync.dma_start(out=q_hbm[rows, j * GROUP:j * GROUP + 2 * D], in_=o_v[:])
+            nc.sync.dma_start(out=q_hbm[rows, j * GROUP + 2 * D:(j + 1) * GROUP], in_=o_s[:])
+
+        new_grouped("x")
+        new_grouped(0)
+        new_grouped(1)
+        spread_scale(1)
+        widen_pass(0, 0, first)
+        spread_scale(2)
+        widen_pass(1, 0, whole)
+        spread_scale(3)
+        widen_pass(0, 1, whole)
+        turn(x_sb[0], grouped_of["x"], 0)
+        widen_pass(1, 1, whole)
+        turn(x_sb[1], grouped_of["x"], 1)
+        widen_pass(0, 2, whole)
+        turn(x_sb[2], grouped_of["x"], 2)
+        widen_pass(1, 2, whole)
+        turn(x_sb[3], grouped_of["x"], 3)
+        widen_pass(0, 3, whole)
+        tables_first_turn()
+        widen_pass(1, 3, whole)
+        tables_second_turn()
+        new_bytes()
+        for r in range(4):
+            load_bytes_rows(3, r)
+        quant_group(0)
+        quant_group("x")
+
+        for j in (0, 1):
+            for r in range(4):
+                multiply(j, r)
+                squares(j, r)
+                widen(j + 2, r)
+                turn_q(j + 2, r)
+            if j == 0:
+                new_grouped(KG)
+            turn(wk_sb[2 * j], grouped_of[KG], 2 * j)
+            turn(wk_sb[2 * j + 1], grouped_of[KG], 2 * j + 1)
+            products(j, 0)
+            add_on(nc.gpsimd, j, 0)
+            products(j, 1)
+            add_on(nc.gpsimd, j, 1)
+            scale_store(j, 0)
+            products(j, 2)
+            scale_store(j, 1)
+            products(j, 3)
+            quant_group(j + 1)
+            if j == 1:
+                quant_group(KG)
+                quant_group(3)
+            add_on(nc.vector, j, 2)
+            add_on(nc.vector, j, 3)
+            if j == 0:
+                scale_store(j, 2)
+                scale_store(j, 3)
+
+        for r in range(4):
+            multiply(2, r)
+            squares(2, r)
+        scale_store(1, 2)
+        scale_store(1, 3)
+        multiply(KG, 0)
+        squares(KG, 0)
+        multiply(KG, 1)
+        squares(KG, 1)
+        products(2, 0)
+        add_on(nc.gpsimd, 2, 0)
+        products(2, 1)
+        add_on(nc.gpsimd, 2, 1)
+        scale_store(2, 0)
+        multiply(KG, 2)
+        squares(KG, 2)
+        products(2, 2)
+        add_on(nc.gpsimd, 2, 2)
+        scale_store(2, 1)
+        multiply(KG, 3)
+        squares(KG, 3)
+        products(2, 3)
+        add_on(nc.gpsimd, 2, 3)
+        scale_store(2, 2)
+        multiply(3, 0)
+        squares(3, 0)
+        products(KG, 0)
+        add_on(nc.gpsimd, KG, 0)
+        multiply(3, 1)
+        squares(3, 1)
+        scale_store(2, 3)
+        products(KG, 1)
+        add_on(nc.gpsimd, KG, 1)
+        multiply(3, 2)
+        squares(3, 2)
+        scale_store(KG, 0)
+        products(KG, 2)
+        add_on(nc.gpsimd, KG, 2)
+        multiply(3, 3)
+        squares(3, 3)
+        scale_store(KG, 1)
+        products(KG, 3)
+        add_on(nc.gpsimd, KG, 3)
+        products(3, 0)
+        add_on(nc.gpsimd, 3, 0)
+        scale_store(KG, 2)
+        products(3, 1)
+        scale_store(KG, 3)
+        products(3, 2)
+        products(3, 3)
+        scale_store(3, 0)
+        add_on(nc.vector, 3, 1)
+        add_on(nc.vector, 3, 2)
+        add_on(nc.vector, 3, 3)
+        scale_store(3, 1)
+        scale_store(3, 2)
+        scale_store_shared(3, 3)

@@ -112,6 +112,10 @@ def tile_qwen3nextattentionforengine_pa_kernel(
             nc.sync.dma_start(out=w_swap[0:HALF, :], in_=col[HALF:D, :])
             nc.sync.dma_start(out=w_swap[HALF:D, :], in_=col[0:HALF, :])
             w_cols.append((w_plain, w_swap))
+        scale_t = keep.tile([P, PASSES, 8], F32, name="scale_t")
+        nc.sync.dma_start(
+            out=scale_t[:, :, 0:4], in_=Wq_query_scale.rearrange("o (g p t) -> p (o g) t", g=PASSES, p=P, t=4)
+        )
         for r in range(4):
             load_bytes_rows(2, r)
         for t in range(4):
@@ -200,6 +204,37 @@ def tile_qwen3nextattentionforengine_pa_kernel(
                     in_=tp[:].rearrange("p s u r -> p s r u"),
                 )
 
+        def cast(j, r):
+            rt = 4 * j + r
+            new_wbf(rt)
+            nc.scalar.copy(out=wbf_of[rt][:], in_=wq_bytes[j][:, r, :].bitcast(FP8))
+
+        turned_of = {}
+
+        def turn_plain(j, r):
+            words = wbf_of[4 * j + r][:].bitcast(F32)
+            banks = []
+            for g0 in (0, 2):
+                tp = psum_t.tile([P, 2, 2, P], F32, name="tp")
+                for gg in range(2):
+                    g = g0 + gg
+                    for u in range(2):
+                        nc.tensor.transpose(tp[:, gg, u, :], words[:, 256 * g + u:256 * (g + 1):2], ident[:])
+                banks.append(tp)
+            turned_of[(j, r)] = banks
+
+        def scale_out(j, r):
+            if r == 0:
+                new_grouped(j)
+            for g in range(PASSES):
+                tp = turned_of[(j, r)][g // 2]
+                nc.vector.tensor_tensor(
+                    out=grouped_of[j][:, g, r * P:(r + 1) * P, :].rearrange("p r (u e) -> p r u e", u=2),
+                    in0=tp[:, g % 2, :, :].bitcast(BF16).rearrange("p u (r e) -> p r u e", e=2),
+                    in1=scale_t[:, g, 0:4].rearrange("p (u e) -> p u e", u=2).unsqueeze(1).to_broadcast([P, P, 2, 2]),
+                    op=ALU.mult,
+                )
+
         def quantize(grouped, codes, scales):
             for g in (0, 2):
                 nc.vector.quantize_mx(
@@ -223,22 +258,9 @@ def tile_qwen3nextattentionforengine_pa_kernel(
                 w_grouped = grp.tile([P, PASSES, GROUP, 4], BF16, name="w_grouped", align_bytes=64)
                 grouped_of[j] = w_grouped
 
-        def widen_piece(rt, c0, c1):
-            nc.vector.tensor_tensor(
-                out=wbf_of[rt][:, c0:c1],
-                in0=wq_bytes[rt // HG][:, rt % HG, c0:c1].bitcast(FP8),
-                in1=scale_bc[:, c0:c1],
-                op=ALU.mult,
-            )
-
         def new_wbf(rt):
             w_bf = wide.tile([P, HID], BF16, name="w_bf")
             wbf_of[rt] = w_bf
-
-        def widen(j, r):
-            rt = 4 * j + r
-            new_wbf(rt)
-            widen_piece(rt, 0, HID)
 
         def widen_pass(j, g, pieces):
             w_bf = wide.tile([P, HID], BF16, name="w_bf")
@@ -253,11 +275,6 @@ def tile_qwen3nextattentionforengine_pa_kernel(
 
         whole = [(r, 0, 512) for r in range(4)]
         first = [(0, 0, 256), (1, 0, 256), (0, 256, 512), (1, 256, 512), (2, 0, 512), (3, 0, 512)]
-
-        def turn_q(j, r):
-            if r == 0:
-                new_grouped(j)
-            turn(wbf_of[4 * j + r], grouped_of[j], r)
 
         def quant_group(j):
             if j == KG or j == "x":
@@ -373,9 +390,13 @@ def tile_qwen3nextattentionforengine_pa_kernel(
         widen_pass(1, 2, whole)
         turn(x_sb[3], grouped_of["x"], 3)
         widen_pass(0, 3, whole)
-        tables_first_turn()
+        cast(2, 0)
         widen_pass(1, 3, whole)
+        cast(2, 1)
+        tables_first_turn()
         tables_second_turn()
+        turn_plain(2, 0)
+        turn_plain(2, 1)
         new_bytes()
         for r in range(4):
             load_bytes_rows(3, r)
@@ -383,32 +404,40 @@ def tile_qwen3nextattentionforengine_pa_kernel(
         quant_group("x")
 
         for j in (0, 1):
-            for r in range(4):
+            n = j + 2
+            for r in range(2):
                 multiply(j, r)
                 squares(j, r)
-                widen(j + 2, r)
-                turn_q(j + 2, r)
+                cast(n, r + 2)
+                scale_out(n, r)
+            for r in (2, 3):
+                multiply(j, r)
+                squares(j, r)
             if j == 0:
                 new_grouped(KG)
             turn(wk_sb[2 * j], grouped_of[KG], 2 * j)
             turn(wk_sb[2 * j + 1], grouped_of[KG], 2 * j + 1)
-            products(j, 0)
-            add_on(nc.gpsimd, j, 0)
-            products(j, 1)
-            add_on(nc.gpsimd, j, 1)
-            scale_store(j, 0)
-            products(j, 2)
-            scale_store(j, 1)
-            products(j, 3)
-            quant_group(j + 1)
-            if j == 1:
-                quant_group(KG)
-                quant_group(3)
-            add_on(nc.vector, j, 2)
-            add_on(nc.vector, j, 3)
+            turn_plain(n, 2)
+            turn_plain(n, 3)
             if j == 0:
+                cast(3, 0)
+                cast(3, 1)
+            for t in range(4):
+                products(j, t)
+                add_on(nc.gpsimd, j, t)
+            scale_store(j, 0)
+            scale_store(j, 1)
+            scale_out(n, 2)
+            scale_out(n, 3)
+            quant_group(j + 1)
+            if j == 0:
+                turn_plain(3, 0)
+                turn_plain(3, 1)
                 scale_store(j, 2)
                 scale_store(j, 3)
+            else:
+                quant_group(KG)
+                quant_group(3)
 
         for r in range(4):
             multiply(2, r)

@@ -39,12 +39,12 @@ def tile_qwen3nextattentionforengine_pa_kernel(
 
     with ExitStack() as ctx:
         keep = ctx.enter_context(tc.tile_pool(name="keep", bufs=1))
-        raw = ctx.enter_context(tc.tile_pool(name="raw", bufs=3))
-        wide = ctx.enter_context(tc.tile_pool(name="wide", bufs=4))
+        raw = ctx.enter_context(tc.tile_pool(name="raw", bufs=8))
+        rows = ctx.enter_context(tc.tile_pool(name="rows", bufs=4))
+        wide = ctx.enter_context(tc.tile_pool(name="wide", bufs=6))
         grp = ctx.enter_context(tc.tile_pool(name="grp", bufs=2))
         epi = ctx.enter_context(tc.tile_pool(name="epi", bufs=8))
         small = ctx.enter_context(tc.tile_pool(name="small", bufs=12))
-        work = ctx.enter_context(tc.tile_pool(name="work", bufs=4))
         psum_t = ctx.enter_context(tc.psum_pool(name="psum_t", bufs=4))
         psum_a = ctx.enter_context(tc.psum_pool(name="psum_a", bufs=4))
         ctx.enter_context(tc.manual_schedule())
@@ -52,10 +52,25 @@ def tile_qwen3nextattentionforengine_pa_kernel(
         cos_sb = keep.tile([P, NT, D], BF16, name="cos_sb")
         sin_sb = keep.tile([P, NT, D], BF16, name="sin_sb")
         scale_bc = keep.tile([P, HID], F32, name="scale_bc")
+        scale_t = keep.tile([P, PASSES, 8], F32, name="scale_t")
 
-        wq_bytes = []
+        wq_bytes = {}
+        wq_group = []
         x_sb = []
         wk_sb = []
+
+        def load_bytes(j, r):
+            rt = HG * j + r
+            wq_raw = raw.tile([P, HID], U8, name="wq_raw")
+            nc.sync.dma_start(out=wq_raw[:], in_=Wq_query_bytes[rt * P:(rt + 1) * P, :])
+            wq_bytes[(j, r)] = wq_raw
+
+        def load_bytes_pass(j, g, r0, r1):
+            cols = slice(g * 512, (g + 1) * 512)
+            nc.sync.dma_start(
+                out=wq_group[j][:, r0:r1, cols],
+                in_=Wq_query_bytes[(HG * j + r0) * P:(HG * j + r1) * P, cols].rearrange("(r p) c -> p r c", p=P),
+            )
 
         def load_scale(c0, c1):
             nc.sync.dma_start(
@@ -63,68 +78,61 @@ def tile_qwen3nextattentionforengine_pa_kernel(
                 in_=Wq_query_scale[0:1, c0:c1].rearrange("o k -> (o k)").partition_broadcast(P),
             )
 
-        def new_bytes():
-            wq_raw = raw.tile([P, HG, HID], U8, name="wq_raw")
-            wq_bytes.append(wq_raw)
+        def load_rows(src, dst, t):
+            row_tile = rows.tile([P, HID], BF16, name="row_tile")
+            nc.sync.dma_start(out=row_tile[:], in_=src[t * P:(t + 1) * P, :])
+            dst.append(row_tile)
 
-        def load_bytes_pass(j, g, r0, r1):
-            cols = slice(g * 512, (g + 1) * 512)
-            nc.sync.dma_start(
-                out=wq_bytes[j][:, r0:r1, cols],
-                in_=Wq_query_bytes[(HG * j + r0) * P:(HG * j + r1) * P, cols].rearrange("(r p) c -> p r c", p=P),
-            )
-
-        def load_bytes_rows(j, r):
-            rt = HG * j + r
-            nc.sync.dma_start(out=wq_bytes[j][:, r, :], in_=Wq_query_bytes[rt * P:(rt + 1) * P, :])
-
-        def load_x(t):
-            xt = keep.tile([P, HID], BF16, name="x_sb%d" % t)
-            nc.sync.dma_start(out=xt[:], in_=x_hbm[t * P:(t + 1) * P, :])
-            x_sb.append(xt)
-
-        for j in range(3):
-            new_bytes()
+        for j in range(2):
+            wq_pair = raw.tile([P, HG, HID], U8, name="wq_pair", bufs=2)
+            wq_group.append(wq_pair)
         load_scale(0, 256)
         load_bytes_pass(0, 0, 0, 2)
         load_scale(256, 512)
         scale_rows = []
         for g in range(1, 4):
-            row = epi.tile([P, GROUP], F32, name="a_sb")
+            row = epi.tile([P, GROUP], F32, name="a_sb", bufs=7)
             nc.vector.memset(row[:], 0.0)
             nc.sync.dma_start(out=row[0:1, :], in_=Wq_query_scale[0:1, g * 512:(g + 1) * 512])
             scale_rows.append(row)
         load_bytes_pass(0, 0, 2, 4)
         load_bytes_pass(1, 0, 0, 4)
-        for g in range(1, 4):
-            load_bytes_pass(0, g, 0, 4)
-            load_bytes_pass(1, g, 0, 4)
-            load_x(g - 1)
-        load_x(3)
-        nc.sync.dma_start(out=cos_sb[:], in_=cos_hbm.rearrange("(t p) d -> p t d", p=P))
-        nc.sync.dma_start(out=sin_sb[:], in_=sin_hbm.rearrange("(t p) d -> p t d", p=P))
-        w_cols = []
-        for w_hbm, nm in ((q_norm_w, "q"), (k_norm_w, "k")):
-            col = w_hbm.rearrange("(d o) -> d o", o=1)
-            w_plain = keep.tile([P, 1], BF16, name="w_plain_" + nm)
-            w_swap = keep.tile([P, 1], BF16, name="w_swap_" + nm)
-            nc.sync.dma_start(out=w_plain[:], in_=col)
-            nc.sync.dma_start(out=w_swap[0:HALF, :], in_=col[HALF:D, :])
-            nc.sync.dma_start(out=w_swap[HALF:D, :], in_=col[0:HALF, :])
-            w_cols.append((w_plain, w_swap))
-        scale_t = keep.tile([P, PASSES, 8], F32, name="scale_t")
+        load_bytes(2, 0)
+        load_bytes_pass(0, 1, 0, 4)
+        load_bytes(2, 1)
+        load_bytes_pass(1, 1, 0, 4)
+        load_rows(x_hbm, x_sb, 0)
+        load_bytes_pass(0, 2, 0, 4)
+        load_rows(x_hbm, x_sb, 1)
+        load_bytes_pass(0, 3, 0, 4)
+        load_bytes_pass(1, 2, 0, 4)
+        load_rows(x_hbm, x_sb, 2)
+        load_bytes_pass(1, 3, 0, 4)
+        load_rows(x_hbm, x_sb, 3)
+        load_bytes(2, 2)
         nc.sync.dma_start(
             out=scale_t[:, :, 0:4], in_=Wq_query_scale.rearrange("o (g p t) -> p (o g) t", g=PASSES, p=P, t=4)
         )
-        for r in range(4):
-            load_bytes_rows(2, r)
-        for t in range(4):
-            wt = keep.tile([P, HID], BF16, name="wk_sb%d" % t)
-            nc.sync.dma_start(out=wt[:], in_=Wk[t * P:(t + 1) * P, :])
-            wk_sb.append(wt)
+        nc.sync.dma_start(out=cos_sb[:], in_=cos_hbm.rearrange("(t p) d -> p t d", p=P))
+        nc.sync.dma_start(out=sin_sb[:], in_=sin_hbm.rearrange("(t p) d -> p t d", p=P))
+        w_plain = []
+        for w_hbm, nm in ((q_norm_w, "q"), (k_norm_w, "k")):
+            w_bc = keep.tile([P, D], BF16, name="w_bc_" + nm)
+            nc.sync.dma_start(out=w_bc[:], in_=w_hbm.partition_broadcast(P))
+            w_plain.append(w_bc)
+        load_rows(Wk, wk_sb, 0)
+        load_bytes(3, 3)
+        load_rows(Wk, wk_sb, 1)
+        load_bytes(2, 3)
+        load_rows(Wk, wk_sb, 2)
+        load_rows(Wk, wk_sb, 3)
+        for r in range(3):
+            load_bytes(3, r)
 
         ident = keep.tile([P, P], F32, name="ident")
         make_identity(nc, ident[:])
+        warm = keep.tile([P, 1], F32, name="warm")
+        nc.scalar.activation(out=warm[:], in_=ident[:, 0:1], func=ACT.Abs_reciprocal_sqrt, bias=1.0)
         ones = keep.tile([P, P], F32, name="ones")
         nc.vector.memset(ones[:], 1.0)
 
@@ -132,53 +140,31 @@ def tile_qwen3nextattentionforengine_pa_kernel(
             spread = psum_t.tile([P, GROUP], F32, name="tp")
             nc.tensor.matmul(out=spread[:], lhsT=ones[:], rhs=scale_rows[g - 1][:], start=True, stop=True)
             nc.scalar.copy(out=scale_bc[:, g * 512:(g + 1) * 512], in_=spread[:])
-        one = keep.tile([P, 1], F32, name="one")
-        nc.gpsimd.memset(one[:], 1.0)
-        warm = keep.tile([P, 1], F32, name="warm")
-        nc.scalar.activation(out=warm[:], in_=one[:], func=ACT.Abs_reciprocal_sqrt)
-
-        ident_bf = keep.tile([P, P], BF16, name="ident_bf")
-        make_identity(nc, ident_bf[:])
-
         tabs = []
         for nm in ("q", "k"):
             tab = keep.tile([P, NT, 2, D], F32, name="tab_" + nm)
             tabs.append(tab)
-        factors = keep.tile([P, 4], F32, name="factors")
-        turned = {}
 
-        def tables_first_turn():
-            for i in range(2):
-                w_plain, w_swap = w_cols[i]
-                nc.scalar.copy(out=factors[:, 2 * i:2 * i + 1], in_=w_plain[:])
-                nc.scalar.activation(
-                    out=factors[0:HALF, 2 * i + 1:2 * i + 2], in_=w_swap[0:HALF, :], func=ACT.Copy, scale=-1.0
+        w_rots = []
+
+        def rotate_weights(i):
+            w_bc = w_plain[i]
+            w_rot = keep.tile([P, D], BF16, name="w_rot_%d" % i)
+            nc.scalar.activation(out=w_rot[:, 0:HALF], in_=w_bc[:, HALF:D], func=ACT.Copy, scale=-1.0)
+            nc.scalar.copy(out=w_rot[:, HALF:D], in_=w_bc[:, 0:HALF])
+            w_rots.append(w_rot)
+
+        def make_table(i):
+            for jj, (src, w) in enumerate(((cos_sb, w_plain[i]), (sin_sb, w_rots[i]))):
+                nc.gpsimd.tensor_tensor(
+                    out=tabs[i][:, :, jj, :], in0=src[:], in1=w[:].unsqueeze(1).to_broadcast([P, NT, D]), op=ALU.mult
                 )
-                nc.scalar.copy(out=factors[HALF:D, 2 * i + 1:2 * i + 2], in_=w_swap[HALF:D, :])
-            for jj, src in enumerate((cos_sb, sin_sb)):
-                tp = psum_t.tile([P, NT, P], BF16, name="tp")
-                for t in range(NT):
-                    nc.tensor.transpose(tp[:, t, :], src[:, t, :], ident_bf[:])
-                for i in range(2):
-                    tab_t = work.tile([P, NT, P], F32, name="tab_t")
-                    nc.scalar.activation(
-                        out=tab_t[:], in_=tp[:], func=ACT.Copy, scale=factors[:, 2 * i + jj:2 * i + jj + 1]
-                    )
-                    turned[(i, jj)] = tab_t
-
-        def tables_second_turn():
-            for i in range(2):
-                for jj in range(2):
-                    tp = psum_t.tile([P, NT, P], F32, name="tp")
-                    for t in range(NT):
-                        nc.tensor.transpose(tp[:, t, :], turned[(i, jj)][:, t, :], ident[:])
-                    nc.scalar.copy(out=tabs[i][:, :, jj, :], in_=tp[:])
 
         KG = NQ
 
-        def turn(src, grouped, slot):
+        def turn(src, j, slot):
             words = src[:].bitcast(F32)
-            gw = grouped[:].bitcast(F32)
+            gw = grouped_of[j][:].bitcast(F32)
             for g0 in (0, 2):
                 tp = psum_t.tile([P, 2, 2, P], F32, name="tp")
                 for gg in range(2):
@@ -204,15 +190,45 @@ def tile_qwen3nextattentionforengine_pa_kernel(
                     in_=tp[:].rearrange("p s u r -> p s r u"),
                 )
 
-        def cast(j, r):
-            rt = 4 * j + r
-            new_wbf(rt)
-            nc.scalar.copy(out=wbf_of[rt][:], in_=wq_bytes[j][:, r, :].bitcast(FP8))
-
+        w_bf_of = {}
+        w_scaled_of = {}
         turned_of = {}
+        grouped_of = {}
+        codes_of = {}
+        acc_of = {}
+        rstd_of = {}
+        ss_of = {}
+        ab_of = {}
+
+        def cast(j, r, pieces=1):
+            w_bf = wide.tile([P, HID], BF16, name="w_bf")
+            n = HID // pieces
+            for c in range(0, HID, n):
+                nc.scalar.copy(out=w_bf[:, c:c + n], in_=wq_bytes[(j, r)][:, c:c + n].bitcast(FP8))
+            w_bf_of[(j, r)] = w_bf
+
+        def scale_on_gpsimd(j, r):
+            w_scaled = wide.tile([P, HID], BF16, name="w_scaled", bufs=2)
+            for c in range(0, HID, HID // 2):
+                nc.gpsimd.tensor_tensor(
+                    out=w_scaled[:, c:c + HID // 2],
+                    in0=w_bf_of[(j, r)][:, c:c + HID // 2],
+                    in1=scale_bc[:, c:c + HID // 2],
+                    op=ALU.mult,
+                )
+            w_scaled_of[(j, r)] = w_scaled
+
+        def widen(j, r):
+            w_bf = wide.tile([P, HID], BF16, name="w_bf")
+            nc.vector.tensor_tensor(out=w_bf[:], in0=wq_bytes[(j, r)][:].bitcast(FP8), in1=scale_bc[:], op=ALU.mult)
+            w_bf_of[(j, r)] = w_bf
+
+        def wait_for_codes(j):
+            word = small.tile([P, 1], U32, name="word")
+            nc.gpsimd.tensor_copy(out=word[:], in_=codes_of[j][0][:, PASSES - 1, GROUP - 1:GROUP])
 
         def turn_plain(j, r):
-            words = wbf_of[4 * j + r][:].bitcast(F32)
+            words = w_bf_of[(j, r)][:].bitcast(F32)
             banks = []
             for g0 in (0, 2):
                 tp = psum_t.tile([P, 2, 2, P], F32, name="tp")
@@ -224,8 +240,6 @@ def tile_qwen3nextattentionforengine_pa_kernel(
             turned_of[(j, r)] = banks
 
         def scale_out(j, r):
-            if r == 0:
-                new_grouped(j)
             for g in range(PASSES):
                 tp = turned_of[(j, r)][g // 2]
                 nc.vector.tensor_tensor(
@@ -235,6 +249,20 @@ def tile_qwen3nextattentionforengine_pa_kernel(
                     op=ALU.mult,
                 )
 
+        def widen_pass(j, g, pieces):
+            w_bf = wide.tile([P, HID], BF16, name="w_bf")
+            for r, c0, c1 in pieces:
+                nc.vector.tensor_tensor(
+                    out=w_bf[:, r * 512 + c0:r * 512 + c1],
+                    in0=wq_group[j][:, r, g * 512 + c0:g * 512 + c1].bitcast(FP8),
+                    in1=scale_bc[:, g * 512 + c0:g * 512 + c1],
+                    op=ALU.mult,
+                )
+            turn_pass(w_bf, grouped_of[j], g)
+
+        whole = [(r, 0, 512) for r in range(4)]
+        first = [(0, 0, 256), (1, 0, 256), (0, 256, 512), (1, 256, 512), (2, 0, 512), (3, 0, 512)]
+
         def quantize(grouped, codes, scales):
             for g in (0, 2):
                 nc.vector.quantize_mx(
@@ -243,13 +271,6 @@ def tile_qwen3nextattentionforengine_pa_kernel(
                     in_=grouped[:, g:g + 2, :, :].rearrange("p g c t -> p (g c t)"),
                 )
 
-        grouped_of = {}
-        codes_of = {}
-        wbf_of = {}
-        acc_of = {}
-        rstd_of = {}
-        ab_of = {}
-
         def new_grouped(j):
             if j == KG or j == "x":
                 xk_grouped = keep.tile([P, PASSES, GROUP, 4], BF16, name="xk_grouped", align_bytes=64)
@@ -257,24 +278,6 @@ def tile_qwen3nextattentionforengine_pa_kernel(
             else:
                 w_grouped = grp.tile([P, PASSES, GROUP, 4], BF16, name="w_grouped", align_bytes=64)
                 grouped_of[j] = w_grouped
-
-        def new_wbf(rt):
-            w_bf = wide.tile([P, HID], BF16, name="w_bf")
-            wbf_of[rt] = w_bf
-
-        def widen_pass(j, g, pieces):
-            w_bf = wide.tile([P, HID], BF16, name="w_bf")
-            for r, c0, c1 in pieces:
-                nc.vector.tensor_tensor(
-                    out=w_bf[:, r * 512 + c0:r * 512 + c1],
-                    in0=wq_bytes[j][:, r, g * 512 + c0:g * 512 + c1].bitcast(FP8),
-                    in1=scale_bc[:, g * 512 + c0:g * 512 + c1],
-                    op=ALU.mult,
-                )
-            turn_pass(w_bf, grouped_of[j], g)
-
-        whole = [(r, 0, 512) for r in range(4)]
-        first = [(0, 0, 256), (1, 0, 256), (0, 256, 512), (1, 256, 512), (2, 0, 512), (3, 0, 512)]
 
         def quant_group(j):
             if j == KG or j == "x":
@@ -289,10 +292,7 @@ def tile_qwen3nextattentionforengine_pa_kernel(
         def multiply(j, t):
             x_codes, x_scales = codes_of["x"]
             w_codes, w_scales = codes_of[j]
-            if j == KG:
-                acc = psum_t.tile([P, GROUP], F32, name="tp")
-            else:
-                acc = psum_a.tile([P, GROUP], F32, name="acc")
+            acc = psum_a.tile([P, GROUP], F32, name="acc")
             toks = slice(t * P, (t + 1) * P)
             for g in range(PASSES):
                 nc.tensor.matmul_mx(
@@ -314,14 +314,17 @@ def tile_qwen3nextattentionforengine_pa_kernel(
                 nc.scalar.activation(
                     out=junk[:], in_=acc[:, h * D:(h + 1) * D], func=ACT.Square, accum_out=ss[:, h:h + 1]
                 )
+            ss_of[(j, t)] = ss
+
+        def norm(j, t):
             rstd = small.tile([P, HG], F32, name="rstd")
-            nc.scalar.activation(out=rstd[:], in_=ss[:], func=ACT.Abs_reciprocal_sqrt, scale=1.0 / D, bias=EPS)
+            nc.scalar.activation(out=rstd[:], in_=ss_of[(j, t)][:], func=ACT.Abs_reciprocal_sqrt, scale=1.0 / D, bias=EPS)
             rstd_of[(j, t)] = rstd
 
         def products(j, t):
             acc = acc_of[(j, t)]
             tab = tabs[1] if j == KG else tabs[0]
-            a_sb = epi.tile([P, GROUP], F32, name="a_sb")
+            a_sb = epi.tile([P, GROUP], F32, name="a_sb", bufs=7)
             b_sb = epi.tile([P, GROUP], F32, name="b_sb", bufs=6)
             nc.vector.tensor_tensor(
                 out=a_sb[:].rearrange("p (h d) -> p h d", d=D),
@@ -378,118 +381,154 @@ def tile_qwen3nextattentionforengine_pa_kernel(
         new_grouped(1)
         spread_scale(1)
         widen_pass(0, 0, first)
+        cast(2, 0)
         spread_scale(2)
         widen_pass(1, 0, whole)
+        cast(2, 1)
         spread_scale(3)
         widen_pass(0, 1, whole)
-        turn(x_sb[0], grouped_of["x"], 0)
+        turn(x_sb[0], "x", 0)
         widen_pass(1, 1, whole)
-        turn(x_sb[1], grouped_of["x"], 1)
+        turn(x_sb[1], "x", 1)
         widen_pass(0, 2, whole)
-        turn(x_sb[2], grouped_of["x"], 2)
-        widen_pass(1, 2, whole)
-        turn(x_sb[3], grouped_of["x"], 3)
         widen_pass(0, 3, whole)
-        cast(2, 0)
+        turn(x_sb[2], "x", 2)
+        widen_pass(1, 2, whole)
+        turn(x_sb[3], "x", 3)
         widen_pass(1, 3, whole)
-        cast(2, 1)
-        tables_first_turn()
-        tables_second_turn()
-        turn_plain(2, 0)
-        turn_plain(2, 1)
-        new_bytes()
-        for r in range(4):
-            load_bytes_rows(3, r)
+        cast(2, 2)
+        rotate_weights(0)
+        rotate_weights(1)
         quant_group(0)
         quant_group("x")
-
-        for j in (0, 1):
-            n = j + 2
-            for r in range(2):
-                multiply(j, r)
-                squares(j, r)
-                cast(n, r + 2)
-                scale_out(n, r)
-            for r in (2, 3):
-                multiply(j, r)
-                squares(j, r)
-            if j == 0:
-                new_grouped(KG)
-            turn(wk_sb[2 * j], grouped_of[KG], 2 * j)
-            turn(wk_sb[2 * j + 1], grouped_of[KG], 2 * j + 1)
-            turn_plain(n, 2)
-            turn_plain(n, 3)
-            if j == 0:
-                cast(3, 0)
-                cast(3, 1)
-            for t in range(4):
-                products(j, t)
-                add_on(nc.gpsimd, j, t)
-            scale_store(j, 0)
-            scale_store(j, 1)
-            scale_out(n, 2)
-            scale_out(n, 3)
-            quant_group(j + 1)
-            if j == 0:
-                turn_plain(3, 0)
-                turn_plain(3, 1)
-                scale_store(j, 2)
-                scale_store(j, 3)
-            else:
-                quant_group(KG)
-                quant_group(3)
-
-        for r in range(4):
-            multiply(2, r)
-            squares(2, r)
-        scale_store(1, 2)
+        new_grouped(2)
+        turn_plain(2, 0)
+        turn_plain(2, 1)
+        wait_for_codes("x")
+        make_table(0)
+        make_table(1)
+        scale_out(2, 0)
+        multiply(0, 0)
+        multiply(0, 1)
+        squares(0, 0)
+        squares(0, 1)
+        norm(0, 0)
+        cast(3, 3)
+        norm(0, 1)
+        scale_out(2, 1)
+        multiply(0, 2)
+        squares(0, 2)
+        multiply(0, 3)
+        squares(0, 3)
+        norm(0, 2)
+        norm(0, 3)
+        turn_plain(2, 2)
+        new_grouped(KG)
+        turn(wk_sb[0], KG, 0)
+        turn(wk_sb[1], KG, 1)
+        turn(wk_sb[2], KG, 2)
+        turn(wk_sb[3], KG, 3)
+        for t in range(4):
+            products(0, t)
+            add_on(nc.gpsimd, 0, t)
+        cast(3, 0)
+        scale_out(2, 2)
+        cast(3, 1)
+        widen(2, 3)
+        turn(w_bf_of[(2, 3)], 2, 3)
+        scale_store(0, 0)
+        scale_store(0, 1)
+        scale_store(0, 2)
+        quant_group(1)
+        quant_group(KG)
+        wait_for_codes(KG)
+        scale_on_gpsimd(3, 3)
+        new_grouped(3)
+        turn_plain(3, 0)
+        turn_plain(3, 1)
+        scale_store(0, 3)
+        scale_out(3, 0)
+        multiply(1, 0)
+        multiply(1, 1)
+        squares(1, 0)
+        squares(1, 1)
+        norm(1, 0)
+        cast(3, 2)
+        norm(1, 1)
+        scale_out(3, 1)
+        multiply(1, 2)
+        squares(1, 2)
+        multiply(1, 3)
+        squares(1, 3)
+        norm(1, 2)
+        norm(1, 3)
+        turn_plain(3, 2)
+        for t in range(4):
+            products(1, t)
+            add_on(nc.gpsimd, 1, t)
+            multiply(KG, t)
+            squares(KG, t)
+            if t > 0:
+                norm(KG, t - 1)
+                scale_store(1, t - 1)
+        scale_out(3, 2)
+        turn(w_scaled_of[(3, 3)], 3, 3)
+        norm(KG, 3)
         scale_store(1, 3)
-        multiply(KG, 0)
-        squares(KG, 0)
-        multiply(KG, 1)
-        squares(KG, 1)
+        for t in range(4):
+            products(KG, t)
+            if t < 2:
+                add_on(nc.gpsimd, KG, t)
+            if t in (1, 2):
+                scale_store(KG, t - 1)
+        add_on(nc.vector, KG, 2)
+        quant_group(2)
+        quant_group(3)
+        multiply(2, 0)
+        squares(2, 0)
+        multiply(2, 1)
+        squares(2, 1)
+        norm(2, 0)
         products(2, 0)
         add_on(nc.gpsimd, 2, 0)
+        add_on(nc.gpsimd, KG, 3)
+        multiply(2, 2)
+        squares(2, 2)
+        norm(2, 1)
         products(2, 1)
         add_on(nc.gpsimd, 2, 1)
         scale_store(2, 0)
-        multiply(KG, 2)
-        squares(KG, 2)
+        multiply(2, 3)
+        squares(2, 3)
+        norm(2, 2)
         products(2, 2)
         add_on(nc.gpsimd, 2, 2)
-        scale_store(2, 1)
-        multiply(KG, 3)
-        squares(KG, 3)
-        products(2, 3)
-        add_on(nc.gpsimd, 2, 3)
-        scale_store(2, 2)
+        scale_store(KG, 2)
+        scale_store(KG, 3)
+        norm(2, 3)
         multiply(3, 0)
         squares(3, 0)
-        products(KG, 0)
-        add_on(nc.gpsimd, KG, 0)
+        products(2, 3)
+        add_on(nc.gpsimd, 2, 3)
+        scale_store(2, 1)
+        norm(3, 0)
         multiply(3, 1)
         squares(3, 1)
-        scale_store(2, 3)
-        products(KG, 1)
-        add_on(nc.gpsimd, KG, 1)
-        multiply(3, 2)
-        squares(3, 2)
-        scale_store(KG, 0)
-        products(KG, 2)
-        add_on(nc.gpsimd, KG, 2)
-        multiply(3, 3)
-        squares(3, 3)
-        scale_store(KG, 1)
-        products(KG, 3)
-        add_on(nc.gpsimd, KG, 3)
         products(3, 0)
         add_on(nc.gpsimd, 3, 0)
-        scale_store(KG, 2)
+        scale_store(2, 2)
+        norm(3, 1)
+        multiply(3, 2)
+        squares(3, 2)
         products(3, 1)
-        scale_store(KG, 3)
+        scale_store(2, 3)
+        norm(3, 2)
+        multiply(3, 3)
+        squares(3, 3)
         products(3, 2)
         products(3, 3)
         scale_store(3, 0)
+        norm(3, 3)
         add_on(nc.vector, 3, 1)
         add_on(nc.vector, 3, 2)
         add_on(nc.vector, 3, 3)

@@ -89,12 +89,15 @@ def tile_qwen3nextattentionforengine_pa_kernel(
         load_scale(0, 256)
         load_bytes_pass(0, 0, 0, 2)
         load_scale(256, 512)
-        scale_rows = []
-        for g in range(1, 4):
-            row = epi.tile([P, GROUP], F32, name="a_sb", bufs=7)
-            nc.vector.memset(row[:], 0.0)
-            nc.sync.dma_start(out=row[0:1, :], in_=Wq_query_scale[0:1, g * 512:(g + 1) * 512])
-            scale_rows.append(row)
+        scale_rows = epi.tile([P, GROUP], F32, name="a_sb", bufs=7)
+        one = keep.tile([P, 1], F32, name="one")
+        warm = keep.tile([P, 1], F32, name="warm")
+        nc.gpsimd.memset(one[:], 1.0)
+        nc.scalar.activation(out=warm[:], in_=one[:], func=ACT.Abs_reciprocal_sqrt)
+        nc.gpsimd.memset(scale_rows[:], 0.0)
+        nc.sync.dma_start(
+            out=scale_rows[0:PASSES, :], in_=Wq_query_scale.rearrange("o (g k) -> (o g) k", g=PASSES)
+        )
         load_bytes_pass(0, 0, 2, 4)
         load_bytes_pass(1, 0, 0, 4)
         load_bytes(2, 0)
@@ -131,14 +134,12 @@ def tile_qwen3nextattentionforengine_pa_kernel(
 
         ident = keep.tile([P, P], F32, name="ident")
         make_identity(nc, ident[:])
-        warm = keep.tile([P, 1], F32, name="warm")
-        nc.scalar.activation(out=warm[:], in_=ident[:, 0:1], func=ACT.Abs_reciprocal_sqrt, bias=1.0)
-        ones = keep.tile([P, P], F32, name="ones")
-        nc.vector.memset(ones[:], 1.0)
 
         def spread_scale(g):
             spread = psum_t.tile([P, GROUP], F32, name="tp")
-            nc.tensor.matmul(out=spread[:], lhsT=ones[:], rhs=scale_rows[g - 1][:], start=True, stop=True)
+            nc.tensor.matmul(
+                out=spread[:], lhsT=ident[:, g:g + 1].to_broadcast([P, P]), rhs=scale_rows[:], start=True, stop=True
+            )
             nc.scalar.copy(out=scale_bc[:, g * 512:(g + 1) * 512], in_=spread[:])
         tabs = []
         for nm in ("q", "k"):

@@ -41,7 +41,7 @@ def tile_qwen3nextattentionforengine_pa_kernel(
         keep = ctx.enter_context(tc.tile_pool(name="keep", bufs=1))
         raw = ctx.enter_context(tc.tile_pool(name="raw", bufs=8))
         rows = ctx.enter_context(tc.tile_pool(name="rows", bufs=4))
-        wide = ctx.enter_context(tc.tile_pool(name="wide", bufs=6))
+        wide = ctx.enter_context(tc.tile_pool(name="wide", bufs=5))
         grp = ctx.enter_context(tc.tile_pool(name="grp", bufs=2))
         epi = ctx.enter_context(tc.tile_pool(name="epi", bufs=8))
         small = ctx.enter_context(tc.tile_pool(name="small", bufs=12))
@@ -49,8 +49,7 @@ def tile_qwen3nextattentionforengine_pa_kernel(
         psum_a = ctx.enter_context(tc.psum_pool(name="psum_a", bufs=4))
         ctx.enter_context(tc.manual_schedule())
 
-        cos_sb = keep.tile([P, NT, D], BF16, name="cos_sb")
-        sin_sb = keep.tile([P, NT, D], BF16, name="sin_sb")
+        cos_sin = keep.tile([P, NT, 2, D], BF16, name="cos_sin")
         scale_bc = keep.tile([P, HID], F32, name="scale_bc")
         scale_t = keep.tile([P, PASSES, 8], F32, name="scale_t")
 
@@ -89,7 +88,7 @@ def tile_qwen3nextattentionforengine_pa_kernel(
         load_scale(0, 256)
         load_bytes_pass(0, 0, 0, 2)
         load_scale(256, 512)
-        scale_rows = epi.tile([P, GROUP], F32, name="a_sb", bufs=7)
+        scale_rows = epi.tile([P, GROUP], F32, name="o_sb", bufs=8)
         one = keep.tile([P, 1], F32, name="one")
         warm = keep.tile([P, 1], F32, name="warm")
         nc.gpsimd.memset(one[:], 1.0)
@@ -98,11 +97,11 @@ def tile_qwen3nextattentionforengine_pa_kernel(
         nc.sync.dma_start(
             out=scale_rows[0:PASSES, :], in_=Wq_query_scale.rearrange("o (g k) -> (o g) k", g=PASSES)
         )
+        load_bytes(2, 0)
         load_bytes_pass(0, 0, 2, 4)
         load_bytes_pass(1, 0, 0, 4)
-        load_bytes(2, 0)
-        load_bytes_pass(0, 1, 0, 4)
         load_bytes(2, 1)
+        load_bytes_pass(0, 1, 0, 4)
         load_bytes_pass(1, 1, 0, 4)
         load_rows(x_hbm, x_sb, 0)
         load_bytes_pass(0, 2, 0, 4)
@@ -116,17 +115,19 @@ def tile_qwen3nextattentionforengine_pa_kernel(
         nc.sync.dma_start(
             out=scale_t[:, :, 0:4], in_=Wq_query_scale.rearrange("o (g p t) -> p (o g) t", g=PASSES, p=P, t=4)
         )
-        nc.sync.dma_start(out=cos_sb[:], in_=cos_hbm.rearrange("(t p) d -> p t d", p=P))
-        nc.sync.dma_start(out=sin_sb[:], in_=sin_hbm.rearrange("(t p) d -> p t d", p=P))
-        w_plain = []
+        nc.sync.dma_start(out=cos_sin[:, :, 0, :], in_=cos_hbm.rearrange("(t p) d -> p t d", p=P))
+        sin_rows = sin_hbm.rearrange("(t p) d -> p t d", p=P)
+        nc.sync.dma_start(out=cos_sin[:, :, 1, 0:HALF], in_=sin_rows[:, :, HALF:D])
+        nc.sync.dma_start(out=cos_sin[:, :, 1, HALF:D], in_=sin_rows[:, :, 0:HALF])
+        w_pairs = []
         for w_hbm, nm in ((q_norm_w, "q"), (k_norm_w, "k")):
-            w_bc = keep.tile([P, D], BF16, name="w_bc_" + nm)
-            nc.sync.dma_start(out=w_bc[:], in_=w_hbm.partition_broadcast(P))
-            w_plain.append(w_bc)
+            w_pair = keep.tile([P, 2, D], BF16, name="w_pair_" + nm)
+            nc.sync.dma_start(out=w_pair[:, 0, :], in_=w_hbm.partition_broadcast(P))
+            w_pairs.append(w_pair)
+        load_bytes(2, 3)
         load_rows(Wk, wk_sb, 0)
         load_bytes(3, 3)
         load_rows(Wk, wk_sb, 1)
-        load_bytes(2, 3)
         load_rows(Wk, wk_sb, 2)
         load_rows(Wk, wk_sb, 3)
         for r in range(3):
@@ -146,20 +147,18 @@ def tile_qwen3nextattentionforengine_pa_kernel(
             tab = keep.tile([P, NT, 2, D], F32, name="tab_" + nm)
             tabs.append(tab)
 
-        w_rots = []
-
         def rotate_weights(i):
-            w_bc = w_plain[i]
-            w_rot = keep.tile([P, D], BF16, name="w_rot_%d" % i)
-            nc.scalar.activation(out=w_rot[:, 0:HALF], in_=w_bc[:, HALF:D], func=ACT.Copy, scale=-1.0)
-            nc.scalar.copy(out=w_rot[:, HALF:D], in_=w_bc[:, 0:HALF])
-            w_rots.append(w_rot)
+            w_pair = w_pairs[i]
+            nc.scalar.copy(out=w_pair[:, 1, 0:HALF], in_=w_pair[:, 0, 0:HALF])
+            nc.scalar.activation(out=w_pair[:, 1, HALF:D], in_=w_pair[:, 0, HALF:D], func=ACT.Copy, scale=-1.0)
 
         def make_table(i):
-            for jj, (src, w) in enumerate(((cos_sb, w_plain[i]), (sin_sb, w_rots[i]))):
-                nc.gpsimd.tensor_tensor(
-                    out=tabs[i][:, :, jj, :], in0=src[:], in1=w[:].unsqueeze(1).to_broadcast([P, NT, D]), op=ALU.mult
-                )
+            nc.gpsimd.tensor_tensor(
+                out=tabs[i][:].rearrange("p t two d -> p t (two d)"),
+                in0=cos_sin[:].rearrange("p t two d -> p t (two d)"),
+                in1=w_pairs[i][:].rearrange("p two d -> p (two d)").unsqueeze(1).to_broadcast([P, NT, 2 * D]),
+                op=ALU.mult,
+            )
 
         KG = NQ
 
@@ -210,19 +209,35 @@ def tile_qwen3nextattentionforengine_pa_kernel(
 
         def scale_on_gpsimd(j, r):
             w_scaled = wide.tile([P, HID], BF16, name="w_scaled", bufs=2)
-            for c in range(0, HID, HID // 2):
-                nc.gpsimd.tensor_tensor(
-                    out=w_scaled[:, c:c + HID // 2],
-                    in0=w_bf_of[(j, r)][:, c:c + HID // 2],
-                    in1=scale_bc[:, c:c + HID // 2],
-                    op=ALU.mult,
-                )
+            nc.gpsimd.tensor_tensor(out=w_scaled[:], in0=w_bf_of[(j, r)][:], in1=scale_bc[:], op=ALU.mult)
             w_scaled_of[(j, r)] = w_scaled
 
         def widen(j, r):
             w_bf = wide.tile([P, HID], BF16, name="w_bf")
             nc.vector.tensor_tensor(out=w_bf[:], in0=wq_bytes[(j, r)][:].bitcast(FP8), in1=scale_bc[:], op=ALU.mult)
             w_bf_of[(j, r)] = w_bf
+
+        def cast_half(j, r):
+            w_bf = wide.tile([P, HID], BF16, name="w_bf")
+            nc.scalar.copy(out=w_bf[:, 0:HID // 2], in_=wq_bytes[(j, r)][:, 0:HID // 2].bitcast(FP8))
+            w_bf_of[(j, r)] = w_bf
+
+        def scale_half_on_gpsimd(j, r):
+            w_scaled = wide.tile([P, HID], BF16, name="w_scaled", bufs=2)
+            half = slice(0, HID // 2)
+            nc.gpsimd.tensor_tensor(
+                out=w_scaled[:, half], in0=w_bf_of[(j, r)][:, half], in1=scale_bc[:, half], op=ALU.mult
+            )
+            w_scaled_of[(j, r)] = w_scaled
+
+        def widen_other_half(j, r):
+            half = slice(HID // 2, HID)
+            nc.vector.tensor_tensor(
+                out=w_scaled_of[(j, r)][:, half],
+                in0=wq_bytes[(j, r)][:, half].bitcast(FP8),
+                in1=scale_bc[:, half],
+                op=ALU.mult,
+            )
 
         def wait_for_codes(j):
             word = small.tile([P, 1], U32, name="word")
@@ -325,28 +340,30 @@ def tile_qwen3nextattentionforengine_pa_kernel(
         def products(j, t):
             acc = acc_of[(j, t)]
             tab = tabs[1] if j == KG else tabs[0]
-            a_sb = epi.tile([P, GROUP], F32, name="a_sb", bufs=7)
-            b_sb = epi.tile([P, GROUP], F32, name="b_sb", bufs=6)
+            if t % 2 == 0:
+                ab_pair = epi.tile([P, 2, 2, GROUP], F32, name="ab_pair", bufs=4)
+                ab_of[(j, t // 2)] = ab_pair
             nc.vector.tensor_tensor(
-                out=a_sb[:].rearrange("p (h d) -> p h d", d=D),
-                in0=tab[:, t, 0, :].unsqueeze(1).to_broadcast([P, HG, D]),
-                in1=acc[:].rearrange("p (h d) -> p h d", d=D),
+                out=ab_of[(j, t // 2)][:, :, t % 2, :].rearrange("p ab (h d) -> p ab h d", d=D),
+                in0=tab[:, t, :, :].unsqueeze(2).to_broadcast([P, 2, HG, D]),
+                in1=acc[:].rearrange("p (h d) -> p h d", d=D).unsqueeze(1).to_broadcast([P, 2, HG, D]),
                 op=ALU.mult,
             )
-            nc.vector.tensor_tensor(
-                out=b_sb[:].rearrange("p (h two d) -> p h two d", two=2, d=HALF),
-                in0=tab[:, t, 1, :].rearrange("p (two d) -> p two d", two=2).unsqueeze(1).to_broadcast([P, HG, 2, HALF]),
-                in1=acc[:].rearrange("p (h two d) -> p h two d", two=2, d=HALF)[:, :, ::-1, :],
-                op=ALU.mult,
-            )
-            ab_of[(j, t)] = (a_sb, b_sb)
 
-        def add_on(engine, j, t):
-            a_sb, b_sb = ab_of[(j, t)]
-            engine.tensor_tensor(out=a_sb[:], in0=a_sb[:], in1=b_sb[:], op=ALU.add)
+        def add_pair(j, pair):
+            ab_pair = ab_of[(j, pair)]
+            a = ab_pair[:, 0, :, :].rearrange("p t (h two d) -> p (t h) two d", two=2, d=HALF)
+            b = ab_pair[:, 1, :, :].rearrange("p t (h two d) -> p (t h) two d", two=2, d=HALF)
+            nc.gpsimd.tensor_tensor(out=a, in0=a, in1=b[:, :, ::-1, :], op=ALU.add)
+
+        def add_one(engine, j, t):
+            ab_pair = ab_of[(j, t // 2)]
+            a = ab_pair[:, 0, t % 2, :].rearrange("p (h two d) -> p h two d", two=2, d=HALF)
+            b = ab_pair[:, 1, t % 2, :].rearrange("p (h two d) -> p h two d", two=2, d=HALF)
+            engine.tensor_tensor(out=a, in0=a, in1=b[:, :, ::-1, :], op=ALU.add)
 
         def scale_store(j, t):
-            a_sb, b_sb = ab_of[(j, t)]
+            a_sb = ab_of[(j, t // 2)][:, 0, t % 2, :]
             rstd = rstd_of[(j, t)]
             o_sb = epi.tile([P, GROUP], F32, name="o_sb", bufs=8)
             for h in range(HG):
@@ -358,34 +375,29 @@ def tile_qwen3nextattentionforengine_pa_kernel(
             else:
                 nc.sync.dma_start(out=q_hbm[rows, j * GROUP:(j + 1) * GROUP], in_=o_sb[:])
 
-        def scale_store_shared(j, t):
-            a_sb, b_sb = ab_of[(j, t)]
+        def scale_store_on_vector(j, t):
+            a_sb = ab_of[(j, t // 2)][:, 0, t % 2, :]
             rstd = rstd_of[(j, t)]
-            o_v = epi.tile([P, GROUP // 2], F32, name="o_v", bufs=1)
-            o_s = epi.tile([P, GROUP // 2], F32, name="o_s", bufs=1)
-            nc.vector.tensor_tensor(
-                out=o_v[:].rearrange("p (h d) -> p h d", d=D),
-                in0=a_sb[:, 0:2 * D].rearrange("p (h d) -> p h d", d=D),
-                in1=rstd[:, 0:2].unsqueeze(2).to_broadcast([P, 2, D]),
-                op=ALU.mult,
-            )
-            for h in (2, 3):
-                nc.scalar.activation(
-                    out=o_s[:, (h - 2) * D:(h - 1) * D], in_=a_sb[:, h * D:(h + 1) * D], func=ACT.Copy, scale=rstd[:, h:h + 1]
-                )
             rows = slice(t * P, (t + 1) * P)
-            nc.sync.dma_start(out=q_hbm[rows, j * GROUP:j * GROUP + 2 * D], in_=o_v[:])
-            nc.sync.dma_start(out=q_hbm[rows, j * GROUP + 2 * D:(j + 1) * GROUP], in_=o_s[:])
+            for h in (0, 2):
+                o_half = epi.tile([P, 2 * D], F32, name="o_half", bufs=2)
+                nc.vector.tensor_tensor(
+                    out=o_half[:].rearrange("p (h d) -> p h d", d=D),
+                    in0=a_sb[:, h * D:(h + 2) * D].rearrange("p (h d) -> p h d", d=D),
+                    in1=rstd[:, h:h + 2].unsqueeze(2).to_broadcast([P, 2, D]),
+                    op=ALU.mult,
+                )
+                nc.sync.dma_start(out=q_hbm[rows, j * GROUP + h * D:j * GROUP + (h + 2) * D], in_=o_half[:])
 
         new_grouped("x")
         new_grouped(0)
         new_grouped(1)
+        cast(2, 0)
         spread_scale(1)
         widen_pass(0, 0, first)
-        cast(2, 0)
+        cast(2, 1)
         spread_scale(2)
         widen_pass(1, 0, whole)
-        cast(2, 1)
         spread_scale(3)
         widen_pass(0, 1, whole)
         turn(x_sb[0], "x", 0)
@@ -394,12 +406,12 @@ def tile_qwen3nextattentionforengine_pa_kernel(
         widen_pass(0, 2, whole)
         widen_pass(0, 3, whole)
         turn(x_sb[2], "x", 2)
+        rotate_weights(0)
+        rotate_weights(1)
         widen_pass(1, 2, whole)
         turn(x_sb[3], "x", 3)
         widen_pass(1, 3, whole)
-        cast(2, 2)
-        rotate_weights(0)
-        rotate_weights(1)
+        cast_half(2, 3)
         quant_group(0)
         quant_group("x")
         new_grouped(2)
@@ -407,10 +419,11 @@ def tile_qwen3nextattentionforengine_pa_kernel(
         turn_plain(2, 1)
         wait_for_codes("x")
         make_table(0)
-        make_table(1)
+        scale_half_on_gpsimd(2, 3)
         scale_out(2, 0)
         multiply(0, 0)
         multiply(0, 1)
+        cast(2, 2)
         squares(0, 0)
         squares(0, 1)
         norm(0, 0)
@@ -429,14 +442,17 @@ def tile_qwen3nextattentionforengine_pa_kernel(
         turn(wk_sb[1], KG, 1)
         turn(wk_sb[2], KG, 2)
         turn(wk_sb[3], KG, 3)
-        for t in range(4):
-            products(0, t)
-            add_on(nc.gpsimd, 0, t)
+        products(0, 0)
+        products(0, 1)
+        add_pair(0, 0)
+        products(0, 2)
+        products(0, 3)
+        add_pair(0, 1)
         cast(3, 0)
         scale_out(2, 2)
         cast(3, 1)
-        widen(2, 3)
-        turn(w_bf_of[(2, 3)], 2, 3)
+        widen_other_half(2, 3)
+        turn(w_scaled_of[(2, 3)], 2, 3)
         scale_store(0, 0)
         scale_store(0, 1)
         scale_store(0, 2)
@@ -444,6 +460,7 @@ def tile_qwen3nextattentionforengine_pa_kernel(
         quant_group(KG)
         wait_for_codes(KG)
         scale_on_gpsimd(3, 3)
+        make_table(1)
         new_grouped(3)
         turn_plain(3, 0)
         turn_plain(3, 1)
@@ -464,25 +481,38 @@ def tile_qwen3nextattentionforengine_pa_kernel(
         norm(1, 2)
         norm(1, 3)
         turn_plain(3, 2)
-        for t in range(4):
-            products(1, t)
-            add_on(nc.gpsimd, 1, t)
-            multiply(KG, t)
-            squares(KG, t)
-            if t > 0:
-                norm(KG, t - 1)
-                scale_store(1, t - 1)
+        products(1, 0)
+        multiply(KG, 0)
+        squares(KG, 0)
+        products(1, 1)
+        add_pair(1, 0)
+        multiply(KG, 1)
+        squares(KG, 1)
+        norm(KG, 0)
+        products(1, 2)
+        multiply(KG, 2)
+        squares(KG, 2)
+        norm(KG, 1)
+        products(1, 3)
+        add_pair(1, 1)
+        scale_store(1, 0)
+        multiply(KG, 3)
+        squares(KG, 3)
+        norm(KG, 2)
+        scale_store(1, 1)
+        norm(KG, 3)
         scale_out(3, 2)
         turn(w_scaled_of[(3, 3)], 3, 3)
-        norm(KG, 3)
+        scale_store(1, 2)
         scale_store(1, 3)
-        for t in range(4):
-            products(KG, t)
-            if t < 2:
-                add_on(nc.gpsimd, KG, t)
-            if t in (1, 2):
-                scale_store(KG, t - 1)
-        add_on(nc.vector, KG, 2)
+        products(KG, 0)
+        add_one(nc.gpsimd, KG, 0)
+        products(KG, 1)
+        add_one(nc.gpsimd, KG, 1)
+        products(KG, 2)
+        products(KG, 3)
+        scale_store(KG, 0)
+        scale_store(KG, 1)
         quant_group(2)
         quant_group(3)
         multiply(2, 0)
@@ -491,48 +521,48 @@ def tile_qwen3nextattentionforengine_pa_kernel(
         squares(2, 1)
         norm(2, 0)
         products(2, 0)
-        add_on(nc.gpsimd, 2, 0)
-        add_on(nc.gpsimd, KG, 3)
+        add_one(nc.gpsimd, 2, 0)
+        add_pair(KG, 1)
         multiply(2, 2)
         squares(2, 2)
         norm(2, 1)
         products(2, 1)
-        add_on(nc.gpsimd, 2, 1)
-        scale_store(2, 0)
+        add_one(nc.gpsimd, 2, 1)
         multiply(2, 3)
         squares(2, 3)
         norm(2, 2)
+        scale_store(2, 0)
         products(2, 2)
-        add_on(nc.gpsimd, 2, 2)
-        scale_store(KG, 2)
-        scale_store(KG, 3)
+        add_one(nc.gpsimd, 2, 2)
         norm(2, 3)
         multiply(3, 0)
         squares(3, 0)
         products(2, 3)
-        add_on(nc.gpsimd, 2, 3)
-        scale_store(2, 1)
-        norm(3, 0)
+        add_one(nc.gpsimd, 2, 3)
         multiply(3, 1)
+        norm(3, 0)
         squares(3, 1)
+        scale_store(KG, 2)
+        scale_store(KG, 3)
         products(3, 0)
-        add_on(nc.gpsimd, 3, 0)
-        scale_store(2, 2)
+        scale_store(2, 1)
         norm(3, 1)
         multiply(3, 2)
         squares(3, 2)
         products(3, 1)
-        scale_store(2, 3)
+        scale_store(2, 2)
         norm(3, 2)
         multiply(3, 3)
         squares(3, 3)
         products(3, 2)
-        products(3, 3)
-        scale_store(3, 0)
         norm(3, 3)
-        add_on(nc.vector, 3, 1)
-        add_on(nc.vector, 3, 2)
-        add_on(nc.vector, 3, 3)
+        products(3, 3)
+        scale_store(2, 3)
+        add_one(nc.vector, 3, 0)
+        scale_store(3, 0)
+        add_one(nc.vector, 3, 1)
         scale_store(3, 1)
+        add_one(nc.vector, 3, 2)
         scale_store(3, 2)
-        scale_store_shared(3, 3)
+        add_one(nc.vector, 3, 3)
+        scale_store_on_vector(3, 3)

@@ -7,6 +7,7 @@ F32 = mybir.dt.float32
 BF16 = mybir.dt.bfloat16
 U32 = mybir.dt.uint32
 U8 = mybir.dt.uint8
+I32 = mybir.dt.int32
 FP8 = mybir.dt.float8_e4m3fn
 FP8X4 = mybir.dt.float8_e4m3fn_x4
 ALU = mybir.AluOpType
@@ -71,12 +72,6 @@ def tile_qwen3nextattentionforengine_pa_kernel(
                 in_=Wq_query_bytes[(HG * j + r0) * P:(HG * j + r1) * P, cols].rearrange("(r p) c -> p r c", p=P),
             )
 
-        def load_scale(c0, c1):
-            nc.sync.dma_start(
-                out=scale_bc[:, c0:c1],
-                in_=Wq_query_scale[0:1, c0:c1].rearrange("o k -> (o k)").partition_broadcast(P),
-            )
-
         def load_rows(src, dst, t):
             row_tile = rows.tile([P, HID], BF16, name="row_tile")
             nc.sync.dma_start(out=row_tile[:], in_=src[t * P:(t + 1) * P, :])
@@ -85,15 +80,15 @@ def tile_qwen3nextattentionforengine_pa_kernel(
         for j in range(2):
             wq_pair = raw.tile([P, HG, HID], U8, name="wq_pair", bufs=2)
             wq_group.append(wq_pair)
-        load_scale(0, 256)
-        load_bytes_pass(0, 0, 0, 2)
-        load_scale(256, 512)
         scale_rows = epi.tile([P, GROUP], F32, name="o_sb", bufs=8)
+        weight_rows = keep.tile([P, 2, D], BF16, name="weight_rows")
+        nc.vector.memset(scale_rows[:].bitcast(I32), 0)
+        nc.vector.memset(weight_rows[:], 0.0)
         one = keep.tile([P, 1], F32, name="one")
         warm = keep.tile([P, 1], F32, name="warm")
         nc.gpsimd.memset(one[:], 1.0)
         nc.scalar.activation(out=warm[:], in_=one[:], func=ACT.Abs_reciprocal_sqrt)
-        nc.gpsimd.memset(scale_rows[:], 0.0)
+        load_bytes_pass(0, 0, 0, 2)
         nc.sync.dma_start(
             out=scale_rows[0:PASSES, :], in_=Wq_query_scale.rearrange("o (g k) -> (o g) k", g=PASSES)
         )
@@ -119,11 +114,8 @@ def tile_qwen3nextattentionforengine_pa_kernel(
         sin_rows = sin_hbm.rearrange("(t p) d -> p t d", p=P)
         nc.sync.dma_start(out=cos_sin[:, :, 1, 0:HALF], in_=sin_rows[:, :, HALF:D])
         nc.sync.dma_start(out=cos_sin[:, :, 1, HALF:D], in_=sin_rows[:, :, 0:HALF])
-        w_pairs = []
-        for w_hbm, nm in ((q_norm_w, "q"), (k_norm_w, "k")):
-            w_pair = keep.tile([P, 2, D], BF16, name="w_pair_" + nm)
-            nc.sync.dma_start(out=w_pair[:, 0, :], in_=w_hbm.partition_broadcast(P))
-            w_pairs.append(w_pair)
+        for i, w_hbm in enumerate((q_norm_w, k_norm_w)):
+            nc.sync.dma_start(out=weight_rows[0:1, i, :], in_=w_hbm.rearrange("(o d) -> o d", o=1))
         load_bytes(2, 3)
         load_rows(Wk, wk_sb, 0)
         load_bytes(3, 3)
@@ -136,27 +128,47 @@ def tile_qwen3nextattentionforengine_pa_kernel(
         ident = keep.tile([P, P], F32, name="ident")
         make_identity(nc, ident[:])
 
-        def spread_scale(g):
-            spread = psum_t.tile([P, GROUP], F32, name="tp")
-            nc.tensor.matmul(
-                out=spread[:], lhsT=ident[:, g:g + 1].to_broadcast([P, P]), rhs=scale_rows[:], start=True, stop=True
-            )
-            nc.scalar.copy(out=scale_bc[:, g * 512:(g + 1) * 512], in_=spread[:])
+        ones = keep.tile([P, P], BF16, name="ones")
+        nc.gpsimd.memset(ones[:], 1.0)
+
+        def spread_scale(g, pieces=1):
+            n = GROUP // pieces
+            for c in range(0, GROUP, n):
+                spread = psum_t.tile([P, n], F32, name="tp")
+                nc.tensor.matmul(
+                    out=spread[:],
+                    lhsT=ident[:, g:g + 1].to_broadcast([P, P]),
+                    rhs=scale_rows[:, c:c + n],
+                    start=True,
+                    stop=True,
+                )
+                nc.scalar.copy(out=scale_bc[:, g * GROUP + c:g * GROUP + c + n], in_=spread[:])
+
         tabs = []
         for nm in ("q", "k"):
             tab = keep.tile([P, NT, 2, D], F32, name="tab_" + nm)
             tabs.append(tab)
 
-        def rotate_weights(i):
-            w_pair = w_pairs[i]
-            nc.scalar.copy(out=w_pair[:, 1, 0:HALF], in_=w_pair[:, 0, 0:HALF])
-            nc.scalar.activation(out=w_pair[:, 1, HALF:D], in_=w_pair[:, 0, HALF:D], func=ACT.Copy, scale=-1.0)
+        w_pairs = keep.tile([P, 2, 2, D], BF16, name="w_pairs")
+
+        def spread_weights():
+            spread = psum_t.tile([P, 2, D], F32, name="tp")
+            nc.tensor.matmul(
+                out=spread[:].rearrange("p i d -> p (i d)"),
+                lhsT=ones[:],
+                rhs=weight_rows[:].rearrange("p i d -> p (i d)"),
+                start=True,
+                stop=True,
+            )
+            nc.scalar.copy(out=w_pairs[:, :, 0, :], in_=spread[:])
+            nc.scalar.copy(out=w_pairs[:, :, 1, 0:HALF], in_=spread[:, :, 0:HALF])
+            nc.scalar.activation(out=w_pairs[:, :, 1, HALF:D], in_=spread[:, :, HALF:D], func=ACT.Copy, scale=-1.0)
 
         def make_table(i):
             nc.gpsimd.tensor_tensor(
                 out=tabs[i][:].rearrange("p t two d -> p t (two d)"),
                 in0=cos_sin[:].rearrange("p t two d -> p t (two d)"),
-                in1=w_pairs[i][:].rearrange("p two d -> p (two d)").unsqueeze(1).to_broadcast([P, NT, 2 * D]),
+                in1=w_pairs[:, i, :, :].rearrange("p two d -> p (two d)").unsqueeze(1).to_broadcast([P, NT, 2 * D]),
                 op=ALU.mult,
             )
 
@@ -392,6 +404,7 @@ def tile_qwen3nextattentionforengine_pa_kernel(
         new_grouped("x")
         new_grouped(0)
         new_grouped(1)
+        spread_scale(0, 2)
         cast(2, 0)
         spread_scale(1)
         widen_pass(0, 0, first)
@@ -406,8 +419,7 @@ def tile_qwen3nextattentionforengine_pa_kernel(
         widen_pass(0, 2, whole)
         widen_pass(0, 3, whole)
         turn(x_sb[2], "x", 2)
-        rotate_weights(0)
-        rotate_weights(1)
+        spread_weights()
         widen_pass(1, 2, whole)
         turn(x_sb[3], "x", 3)
         widen_pass(1, 3, whole)

@@ -80,20 +80,21 @@ def tile_qwen3nextattentionforengine_pa_kernel(
         for j in range(2):
             wq_pair = raw.tile([P, HG, HID], U8, name="wq_pair", bufs=2)
             wq_group.append(wq_pair)
-        scale_rows = epi.tile([P, GROUP], F32, name="o_sb", bufs=8)
+        scale_rows = epi.tile([P, GROUP], F32, name="o_sb", bufs=7)
         weight_rows = keep.tile([P, 2, D], BF16, name="weight_rows")
+        zeros = keep.tile([P, P], BF16, name="zeros")
+        nc.vector.memset(zeros[:], 0.0)
         nc.vector.memset(scale_rows[:].bitcast(I32), 0)
         nc.vector.memset(weight_rows[:], 0.0)
         one = keep.tile([P, 1], F32, name="one")
         warm = keep.tile([P, 1], F32, name="warm")
         nc.gpsimd.memset(one[:], 1.0)
         nc.scalar.activation(out=warm[:], in_=one[:], func=ACT.Abs_reciprocal_sqrt)
-        load_bytes_pass(0, 0, 0, 2)
         nc.sync.dma_start(
             out=scale_rows[0:PASSES, :], in_=Wq_query_scale.rearrange("o (g k) -> (o g) k", g=PASSES)
         )
+        load_bytes_pass(0, 0, 0, 4)
         load_bytes(2, 0)
-        load_bytes_pass(0, 0, 2, 4)
         load_bytes_pass(1, 0, 0, 4)
         load_bytes(2, 1)
         load_bytes_pass(0, 1, 0, 4)
@@ -131,18 +132,30 @@ def tile_qwen3nextattentionforengine_pa_kernel(
         ones = keep.tile([P, P], BF16, name="ones")
         nc.gpsimd.memset(ones[:], 1.0)
 
-        def spread_scale(g, pieces=1):
-            n = GROUP // pieces
-            for c in range(0, GROUP, n):
-                spread = psum_t.tile([P, n], F32, name="tp")
+        def warm_up():
+            idle = psum_a.tile([P, GROUP], F32, name="acc")
+            for n in range(4):
                 nc.tensor.matmul(
-                    out=spread[:],
-                    lhsT=ident[:, g:g + 1].to_broadcast([P, P]),
-                    rhs=scale_rows[:, c:c + n],
+                    out=idle[:],
+                    lhsT=zeros[:],
+                    rhs=zeros[:].unsqueeze(1).to_broadcast([P, HG, P]),
                     start=True,
                     stop=True,
                 )
-                nc.scalar.copy(out=scale_bc[:, g * GROUP + c:g * GROUP + c + n], in_=spread[:])
+
+        first_cuts = ((0, 128), (128, 256), (256, GROUP))
+
+        def spread_scale(g, cuts=((0, GROUP),)):
+            for c0, c1 in cuts:
+                spread = psum_t.tile([P, c1 - c0], F32, name="tp")
+                nc.tensor.matmul(
+                    out=spread[:],
+                    lhsT=ident[:, g:g + 1].to_broadcast([P, P]),
+                    rhs=scale_rows[:, c0:c1],
+                    start=True,
+                    stop=True,
+                )
+                nc.scalar.copy(out=scale_bc[:, g * GROUP + c0:g * GROUP + c1], in_=spread[:])
 
         tabs = []
         for nm in ("q", "k"):
@@ -289,7 +302,7 @@ def tile_qwen3nextattentionforengine_pa_kernel(
             turn_pass(w_bf, grouped_of[j], g)
 
         whole = [(r, 0, 512) for r in range(4)]
-        first = [(0, 0, 256), (1, 0, 256), (0, 256, 512), (1, 256, 512), (2, 0, 512), (3, 0, 512)]
+        first = [(r, c0, c1) for c0, c1 in first_cuts for r in range(HG)]
 
         def quantize(grouped, codes, scales):
             for g in (0, 2):
@@ -377,7 +390,7 @@ def tile_qwen3nextattentionforengine_pa_kernel(
         def scale_store(j, t):
             a_sb = ab_of[(j, t // 2)][:, 0, t % 2, :]
             rstd = rstd_of[(j, t)]
-            o_sb = epi.tile([P, GROUP], F32, name="o_sb", bufs=8)
+            o_sb = epi.tile([P, GROUP], F32, name="o_sb", bufs=7)
             for h in range(HG):
                 hs = slice(h * D, (h + 1) * D)
                 nc.scalar.activation(out=o_sb[:, hs], in_=a_sb[:, hs], func=ACT.Copy, scale=rstd[:, h:h + 1])
@@ -404,7 +417,8 @@ def tile_qwen3nextattentionforengine_pa_kernel(
         new_grouped("x")
         new_grouped(0)
         new_grouped(1)
-        spread_scale(0, 2)
+        warm_up()
+        spread_scale(0, first_cuts)
         cast(2, 0)
         spread_scale(1)
         widen_pass(0, 0, first)

@@ -80,20 +80,21 @@ def tile_qwen3nextattentionforengine_pa_kernel(
         for j in range(2):
             wq_pair = raw.tile([P, HG, HID], U8, name="wq_pair", bufs=2)
             wq_group.append(wq_pair)
-        scale_rows = epi.tile([P, GROUP], F32, name="o_sb", bufs=7)
+        scale_rows = epi.tile([P, GROUP], F32, name="o_sb", bufs=5)
         weight_rows = keep.tile([P, 2, D], BF16, name="weight_rows")
         zeros = keep.tile([P, P], BF16, name="zeros")
-        nc.vector.memset(zeros[:], 0.0)
         nc.vector.memset(scale_rows[:].bitcast(I32), 0)
+        nc.vector.memset(zeros[:], 0.0)
         nc.vector.memset(weight_rows[:], 0.0)
         one = keep.tile([P, 1], F32, name="one")
         warm = keep.tile([P, 1], F32, name="warm")
         nc.gpsimd.memset(one[:], 1.0)
         nc.scalar.activation(out=warm[:], in_=one[:], func=ACT.Abs_reciprocal_sqrt)
+        load_bytes_pass(0, 0, 0, 2)
         nc.sync.dma_start(
             out=scale_rows[0:PASSES, :], in_=Wq_query_scale.rearrange("o (g k) -> (o g) k", g=PASSES)
         )
-        load_bytes_pass(0, 0, 0, 4)
+        load_bytes_pass(0, 0, 2, 4)
         load_bytes(2, 0)
         load_bytes_pass(1, 0, 0, 4)
         load_bytes(2, 1)
@@ -366,13 +367,35 @@ def tile_qwen3nextattentionforengine_pa_kernel(
             acc = acc_of[(j, t)]
             tab = tabs[1] if j == KG else tabs[0]
             if t % 2 == 0:
-                ab_pair = epi.tile([P, 2, 2, GROUP], F32, name="ab_pair", bufs=4)
+                ab_pair = epi.tile([P, 2, 2, GROUP], F32, name="ab_pair", bufs=5)
                 ab_of[(j, t // 2)] = ab_pair
             nc.vector.tensor_tensor(
                 out=ab_of[(j, t // 2)][:, :, t % 2, :].rearrange("p ab (h d) -> p ab h d", d=D),
                 in0=tab[:, t, :, :].unsqueeze(2).to_broadcast([P, 2, HG, D]),
                 in1=acc[:].rearrange("p (h d) -> p h d", d=D).unsqueeze(1).to_broadcast([P, 2, HG, D]),
                 op=ALU.mult,
+            )
+
+        def products_scaled(j, t):
+            acc = acc_of[(j, t)]
+            rstd = rstd_of[(j, t)]
+            if t % 2 == 0:
+                ab_pair = epi.tile([P, 2, 2, GROUP], F32, name="ab_pair", bufs=5)
+                ab_of[(j, t // 2)] = ab_pair
+            for h in range(HG):
+                hs = slice(h * D, (h + 1) * D)
+                nc.vector.scalar_tensor_tensor(
+                    out=ab_of[(j, t // 2)][:, :, t % 2, hs],
+                    in0=acc[:, hs].unsqueeze(1).to_broadcast([P, 2, D]),
+                    scalar=rstd[:, h:h + 1],
+                    in1=tabs[0][:, t, :, :],
+                    op0=ALU.mult,
+                    op1=ALU.mult,
+                )
+
+        def store_sum(j, t):
+            nc.sync.dma_start(
+                out=q_hbm[t * P:(t + 1) * P, j * GROUP:(j + 1) * GROUP], in_=ab_of[(j, t // 2)][:, 0, t % 2, :]
             )
 
         def add_pair(j, pair):
@@ -390,7 +413,7 @@ def tile_qwen3nextattentionforengine_pa_kernel(
         def scale_store(j, t):
             a_sb = ab_of[(j, t // 2)][:, 0, t % 2, :]
             rstd = rstd_of[(j, t)]
-            o_sb = epi.tile([P, GROUP], F32, name="o_sb", bufs=7)
+            o_sb = epi.tile([P, GROUP], F32, name="o_sb", bufs=5)
             for h in range(HG):
                 hs = slice(h * D, (h + 1) * D)
                 nc.scalar.activation(out=o_sb[:, hs], in_=a_sb[:, hs], func=ACT.Copy, scale=rstd[:, h:h + 1])
@@ -399,20 +422,6 @@ def tile_qwen3nextattentionforengine_pa_kernel(
                 nc.sync.dma_start(out=k_hbm[rows, :], in_=o_sb[:])
             else:
                 nc.sync.dma_start(out=q_hbm[rows, j * GROUP:(j + 1) * GROUP], in_=o_sb[:])
-
-        def scale_store_on_vector(j, t):
-            a_sb = ab_of[(j, t // 2)][:, 0, t % 2, :]
-            rstd = rstd_of[(j, t)]
-            rows = slice(t * P, (t + 1) * P)
-            for h in (0, 2):
-                o_half = epi.tile([P, 2 * D], F32, name="o_half", bufs=2)
-                nc.vector.tensor_tensor(
-                    out=o_half[:].rearrange("p (h d) -> p h d", d=D),
-                    in0=a_sb[:, h * D:(h + 2) * D].rearrange("p (h d) -> p h d", d=D),
-                    in1=rstd[:, h:h + 2].unsqueeze(2).to_broadcast([P, 2, D]),
-                    op=ALU.mult,
-                )
-                nc.sync.dma_start(out=q_hbm[rows, j * GROUP + h * D:j * GROUP + (h + 2) * D], in_=o_half[:])
 
         new_grouped("x")
         new_grouped(0)
@@ -568,27 +577,27 @@ def tile_qwen3nextattentionforengine_pa_kernel(
         multiply(3, 1)
         norm(3, 0)
         squares(3, 1)
-        scale_store(KG, 2)
-        scale_store(KG, 3)
-        products(3, 0)
-        scale_store(2, 1)
-        norm(3, 1)
         multiply(3, 2)
+        norm(3, 1)
+        products_scaled(3, 0)
         squares(3, 2)
-        products(3, 1)
-        scale_store(2, 2)
-        norm(3, 2)
         multiply(3, 3)
+        norm(3, 2)
+        products_scaled(3, 1)
         squares(3, 3)
-        products(3, 2)
+        scale_store(KG, 2)
         norm(3, 3)
-        products(3, 3)
-        scale_store(2, 3)
+        scale_store(KG, 3)
+        products_scaled(3, 2)
+        scale_store(2, 1)
+        products_scaled(3, 3)
+        scale_store(2, 2)
         add_one(nc.vector, 3, 0)
-        scale_store(3, 0)
+        store_sum(3, 0)
+        scale_store(2, 3)
         add_one(nc.vector, 3, 1)
-        scale_store(3, 1)
+        store_sum(3, 1)
         add_one(nc.vector, 3, 2)
-        scale_store(3, 2)
+        store_sum(3, 2)
         add_one(nc.vector, 3, 3)
-        scale_store_on_vector(3, 3)
+        store_sum(3, 3)

from contextlib import ExitStack

import concourse.mybir as mybir
from concourse.masks import make_identity

F32 = mybir.dt.float32
BF16 = mybir.dt.bfloat16
U32 = mybir.dt.uint32
U8 = mybir.dt.uint8
I32 = mybir.dt.int32
FP8 = mybir.dt.float8_e4m3fn
FP8X4 = mybir.dt.float8_e4m3fn_x4
ALU = mybir.AluOpType
ACT = mybir.ActivationFunctionType

P = 128
TOK = 512
HID = 2048
D = 128
HALF = 64
PASSES = 4
NT = 4
GROUP = 512
HG = 4
NQ = 4
EPS = 1e-6

FLOPS = 2 * TOK * HID * (2048 + 512)


def tile_qwen3nextattentionforengine_pa_kernel(
    tc, hidden_states, cos, sin, Wq_query_bytes, Wq_query_scale, Wk, q_norm_w, k_norm_w, out_0, out_1
):
    nc = tc.nc
    x_hbm = hidden_states.flatten_outer_dims()
    cos_hbm = cos.flatten_outer_dims()
    sin_hbm = sin.flatten_outer_dims()
    q_hbm = out_0.rearrange("b s h d -> (b s) (h d)")
    k_hbm = out_1.rearrange("b s h d -> (b s) (h d)")

    with ExitStack() as ctx:
        keep = ctx.enter_context(tc.tile_pool(name="keep", bufs=1))
        raw = ctx.enter_context(tc.tile_pool(name="raw", bufs=8))
        rows = ctx.enter_context(tc.tile_pool(name="rows", bufs=4))
        wide = ctx.enter_context(tc.tile_pool(name="wide", bufs=5))
        grp = ctx.enter_context(tc.tile_pool(name="grp", bufs=2))
        epi = ctx.enter_context(tc.tile_pool(name="epi", bufs=8))
        small = ctx.enter_context(tc.tile_pool(name="small", bufs=12))
        psum_t = ctx.enter_context(tc.psum_pool(name="psum_t", bufs=4))
        psum_a = ctx.enter_context(tc.psum_pool(name="psum_a", bufs=4))
        ctx.enter_context(tc.manual_schedule())

        cos_sin = keep.tile([P, NT, 2, D], BF16, name="cos_sin")
        scale_bc = keep.tile([P, HID], F32, name="scale_bc")
        scale_t = keep.tile([P, PASSES, 8], F32, name="scale_t")

        wq_bytes = {}
        wq_group = []
        x_sb = []
        wk_sb = []

        def load_bytes(j, r):
            rt = HG * j + r
            wq_raw = raw.tile([P, HID], U8, name="wq_raw")
            nc.sync.dma_start(out=wq_raw[:], in_=Wq_query_bytes[rt * P:(rt + 1) * P, :])
            wq_bytes[(j, r)] = wq_raw

        def load_bytes_pass(j, g, r0, r1):
            cols = slice(g * 512, (g + 1) * 512)
            nc.sync.dma_start(
                out=wq_group[j][:, r0:r1, cols],
                in_=Wq_query_bytes[(HG * j + r0) * P:(HG * j + r1) * P, cols].rearrange("(r p) c -> p r c", p=P),
            )

        def load_rows(src, dst, t):
            row_tile = rows.tile([P, HID], BF16, name="row_tile")
            nc.sync.dma_start(out=row_tile[:], in_=src[t * P:(t + 1) * P, :])
            dst.append(row_tile)

        for j in range(2):
            wq_pair = raw.tile([P, HG, HID], U8, name="wq_pair", bufs=2)
            wq_group.append(wq_pair)
        scale_rows = epi.tile([P, GROUP], F32, name="o_sb", bufs=5)
        weight_rows = keep.tile([P, 2, D], BF16, name="weight_rows")
        zeros = keep.tile([P, P], BF16, name="zeros")
        nc.vector.memset(scale_rows[:].bitcast(I32), 0)
        nc.vector.memset(zeros[:], 0.0)
        nc.vector.memset(weight_rows[:], 0.0)
        one = keep.tile([P, 1], F32, name="one")
        warm = keep.tile([P, 1], F32, name="warm")
        nc.gpsimd.memset(one[:], 1.0)
        nc.scalar.activation(out=warm[:], in_=one[:], func=ACT.Abs_reciprocal_sqrt)
        load_bytes_pass(0, 0, 0, 2)
        nc.sync.dma_start(
            out=scale_rows[0:PASSES, :], in_=Wq_query_scale.rearrange("o (g k) -> (o g) k", g=PASSES)
        )
        load_bytes_pass(0, 0, 2, 4)
        load_bytes(2, 0)
        load_bytes_pass(1, 0, 0, 4)
        load_bytes(2, 1)
        load_bytes_pass(0, 1, 0, 4)
        load_bytes_pass(1, 1, 0, 4)
        load_rows(x_hbm, x_sb, 0)
        load_bytes_pass(0, 2, 0, 4)
        load_rows(x_hbm, x_sb, 1)
        load_bytes_pass(0, 3, 0, 4)
        load_bytes_pass(1, 2, 0, 4)
        load_rows(x_hbm, x_sb, 2)
        load_bytes_pass(1, 3, 0, 4)
        load_rows(x_hbm, x_sb, 3)
        load_bytes(2, 2)
        nc.sync.dma_start(
            out=scale_t[:, :, 0:4], in_=Wq_query_scale.rearrange("o (g p t) -> p (o g) t", g=PASSES, p=P, t=4)
        )
        nc.sync.dma_start(out=cos_sin[:, :, 0, :], in_=cos_hbm.rearrange("(t p) d -> p t d", p=P))
        sin_rows = sin_hbm.rearrange("(t p) d -> p t d", p=P)
        nc.sync.dma_start(out=cos_sin[:, :, 1, 0:HALF], in_=sin_rows[:, :, HALF:D])
        nc.sync.dma_start(out=cos_sin[:, :, 1, HALF:D], in_=sin_rows[:, :, 0:HALF])
        for i, w_hbm in enumerate((q_norm_w, k_norm_w)):
            nc.sync.dma_start(out=weight_rows[0:1, i, :], in_=w_hbm.rearrange("(o d) -> o d", o=1))
        load_bytes(2, 3)
        load_rows(Wk, wk_sb, 0)
        load_bytes(3, 3)
        load_rows(Wk, wk_sb, 1)
        load_rows(Wk, wk_sb, 2)
        load_rows(Wk, wk_sb, 3)
        for r in range(3):
            load_bytes(3, r)

        ident = keep.tile([P, P], F32, name="ident")
        make_identity(nc, ident[:])

        ones = keep.tile([P, P], BF16, name="ones")
        nc.gpsimd.memset(ones[:], 1.0)

        def warm_up():
            idle = psum_a.tile([P, GROUP], F32, name="acc")
            for n in range(4):
                nc.tensor.matmul(
                    out=idle[:],
                    lhsT=zeros[:],
                    rhs=zeros[:].unsqueeze(1).to_broadcast([P, HG, P]),
                    start=True,
                    stop=True,
                )

        first_cuts = ((0, 128), (128, 256), (256, GROUP))

        def spread_scale(g, cuts=((0, GROUP),)):
            for c0, c1 in cuts:
                spread = psum_t.tile([P, c1 - c0], F32, name="tp")
                nc.tensor.matmul(
                    out=spread[:],
                    lhsT=ident[:, g:g + 1].to_broadcast([P, P]),
                    rhs=scale_rows[:, c0:c1],
                    start=True,
                    stop=True,
                )
                nc.scalar.copy(out=scale_bc[:, g * GROUP + c0:g * GROUP + c1], in_=spread[:])

        tabs = []
        for nm in ("q", "k"):
            tab = keep.tile([P, NT, 2, D], F32, name="tab_" + nm)
            tabs.append(tab)

        w_pairs = keep.tile([P, 2, 2, D], BF16, name="w_pairs")

        def spread_weights():
            spread = psum_t.tile([P, 2, D], F32, name="tp")
            nc.tensor.matmul(
                out=spread[:].rearrange("p i d -> p (i d)"),
                lhsT=ones[:],
                rhs=weight_rows[:].rearrange("p i d -> p (i d)"),
                start=True,
                stop=True,
            )
            nc.scalar.copy(out=w_pairs[:, :, 0, :], in_=spread[:])
            nc.scalar.copy(out=w_pairs[:, :, 1, 0:HALF], in_=spread[:, :, 0:HALF])
            nc.scalar.activation(out=w_pairs[:, :, 1, HALF:D], in_=spread[:, :, HALF:D], func=ACT.Copy, scale=-1.0)

        def make_table(i):
            nc.gpsimd.tensor_tensor(
                out=tabs[i][:].rearrange("p t two d -> p t (two d)"),
                in0=cos_sin[:].rearrange("p t two d -> p t (two d)"),
                in1=w_pairs[:, i, :, :].rearrange("p two d -> p (two d)").unsqueeze(1).to_broadcast([P, NT, 2 * D]),
                op=ALU.mult,
            )

        KG = NQ

        def turn(src, j, slot):
            words = src[:].bitcast(F32)
            gw = grouped_of[j][:].bitcast(F32)
            for g0 in (0, 2):
                tp = psum_t.tile([P, 2, 2, P], F32, name="tp")
                for gg in range(2):
                    g = g0 + gg
                    for u in range(2):
                        nc.tensor.transpose(tp[:, gg, u, :], words[:, 256 * g + u:256 * (g + 1):2], ident[:])
                nc.scalar.copy(
                    out=gw[:, g0:g0 + 2, slot * P:(slot + 1) * P, :],
                    in_=tp[:].rearrange("p g u r -> p g r u"),
                )

        def turn_pass(src, grouped, g):
            words = src[:].bitcast(F32)
            gw = grouped[:].bitcast(F32)
            for r0 in (0, 2):
                tp = psum_t.tile([P, 2, 2, P], F32, name="tp")
                for rr in range(2):
                    r = r0 + rr
                    for u in range(2):
                        nc.tensor.transpose(tp[:, rr, u, :], words[:, 256 * r + u:256 * (r + 1):2], ident[:])
                nc.scalar.copy(
                    out=gw[:, g, r0 * P:(r0 + 2) * P, :].rearrange("p (s r) u -> p s r u", s=2),
                    in_=tp[:].rearrange("p s u r -> p s r u"),
                )

        w_bf_of = {}
        w_scaled_of = {}
        turned_of = {}
        grouped_of = {}
        codes_of = {}
        acc_of = {}
        rstd_of = {}
        ss_of = {}
        ab_of = {}

        def cast(j, r, pieces=1):
            w_bf = wide.tile([P, HID], BF16, name="w_bf")
            n = HID // pieces
            for c in range(0, HID, n):
                nc.scalar.copy(out=w_bf[:, c:c + n], in_=wq_bytes[(j, r)][:, c:c + n].bitcast(FP8))
            w_bf_of[(j, r)] = w_bf

        def scale_on_gpsimd(j, r):
            w_scaled = wide.tile([P, HID], BF16, name="w_scaled", bufs=2)
            nc.gpsimd.tensor_tensor(out=w_scaled[:], in0=w_bf_of[(j, r)][:], in1=scale_bc[:], op=ALU.mult)
            w_scaled_of[(j, r)] = w_scaled

        def widen(j, r):
            w_bf = wide.tile([P, HID], BF16, name="w_bf")
            nc.vector.tensor_tensor(out=w_bf[:], in0=wq_bytes[(j, r)][:].bitcast(FP8), in1=scale_bc[:], op=ALU.mult)
            w_bf_of[(j, r)] = w_bf

        def cast_half(j, r):
            w_bf = wide.tile([P, HID], BF16, name="w_bf")
            nc.scalar.copy(out=w_bf[:, 0:HID // 2], in_=wq_bytes[(j, r)][:, 0:HID // 2].bitcast(FP8))
            w_bf_of[(j, r)] = w_bf

        def scale_half_on_gpsimd(j, r):
            w_scaled = wide.tile([P, HID], BF16, name="w_scaled", bufs=2)
            half = slice(0, HID // 2)
            nc.gpsimd.tensor_tensor(
                out=w_scaled[:, half], in0=w_bf_of[(j, r)][:, half], in1=scale_bc[:, half], op=ALU.mult
            )
            w_scaled_of[(j, r)] = w_scaled

        def widen_other_half(j, r):
            half = slice(HID // 2, HID)
            nc.vector.tensor_tensor(
                out=w_scaled_of[(j, r)][:, half],
                in0=wq_bytes[(j, r)][:, half].bitcast(FP8),
                in1=scale_bc[:, half],
                op=ALU.mult,
            )

        def wait_for_codes(j):
            word = small.tile([P, 1], U32, name="word")
            nc.gpsimd.tensor_copy(out=word[:], in_=codes_of[j][0][:, PASSES - 1, GROUP - 1:GROUP])

        def turn_plain(j, r):
            words = w_bf_of[(j, r)][:].bitcast(F32)
            banks = []
            for g0 in (0, 2):
                tp = psum_t.tile([P, 2, 2, P], F32, name="tp")
                for gg in range(2):
                    g = g0 + gg
                    for u in range(2):
                        nc.tensor.transpose(tp[:, gg, u, :], words[:, 256 * g + u:256 * (g + 1):2], ident[:])
                banks.append(tp)
            turned_of[(j, r)] = banks

        def scale_out(j, r):
            for g in range(PASSES):
                tp = turned_of[(j, r)][g // 2]
                nc.vector.tensor_tensor(
                    out=grouped_of[j][:, g, r * P:(r + 1) * P, :].rearrange("p r (u e) -> p r u e", u=2),
                    in0=tp[:, g % 2, :, :].bitcast(BF16).rearrange("p u (r e) -> p r u e", e=2),
                    in1=scale_t[:, g, 0:4].rearrange("p (u e) -> p u e", u=2).unsqueeze(1).to_broadcast([P, P, 2, 2]),
                    op=ALU.mult,
                )

        def widen_pass(j, g, pieces):
            w_bf = wide.tile([P, HID], BF16, name="w_bf")
            for r, c0, c1 in pieces:
                nc.vector.tensor_tensor(
                    out=w_bf[:, r * 512 + c0:r * 512 + c1],
                    in0=wq_group[j][:, r, g * 512 + c0:g * 512 + c1].bitcast(FP8),
                    in1=scale_bc[:, g * 512 + c0:g * 512 + c1],
                    op=ALU.mult,
                )
            turn_pass(w_bf, grouped_of[j], g)

        whole = [(r, 0, 512) for r in range(4)]
        first = [(r, c0, c1) for c0, c1 in first_cuts for r in range(HG)]

        def quantize(grouped, codes, scales):
            for g in (0, 2):
                nc.vector.quantize_mx(
                    out=codes[:, g:g + 2, :].rearrange("p g c -> p (g c)").bitcast(FP8X4),
                    scales=scales[:, g:g + 2, :].rearrange("p g c -> p (g c)"),
                    in_=grouped[:, g:g + 2, :, :].rearrange("p g c t -> p (g c t)"),
                )

        def new_grouped(j):
            if j == KG or j == "x":
                xk_grouped = keep.tile([P, PASSES, GROUP, 4], BF16, name="xk_grouped", align_bytes=64)
                grouped_of[j] = xk_grouped
            else:
                w_grouped = grp.tile([P, PASSES, GROUP, 4], BF16, name="w_grouped", align_bytes=64)
                grouped_of[j] = w_grouped

        def quant_group(j):
            if j == KG or j == "x":
                codes = keep.tile([P, PASSES, GROUP], U32, name="codes_%s" % j, align_bytes=64)
                scales = keep.tile([P, PASSES, GROUP], U8, name="scales_%s" % j, align_bytes=64)
            else:
                codes = grp.tile([P, PASSES, GROUP], U32, name="w_codes", align_bytes=64)
                scales = grp.tile([P, PASSES, GROUP], U8, name="w_scales", align_bytes=64)
            quantize(grouped_of[j], codes, scales)
            codes_of[j] = (codes, scales)

        def multiply(j, t):
            x_codes, x_scales = codes_of["x"]
            w_codes, w_scales = codes_of[j]
            acc = psum_a.tile([P, GROUP], F32, name="acc")
            toks = slice(t * P, (t + 1) * P)
            for g in range(PASSES):
                nc.tensor.matmul_mx(
                    out=acc[:],
                    lhsT=x_codes[:, g, toks].bitcast(FP8X4),
                    lhsT_scale=x_scales[:, g, toks],
                    rhs=w_codes[:, g, :].bitcast(FP8X4),
                    rhs_scale=w_scales[:, g, :],
                    start=(g == 0),
                    stop=(g == PASSES - 1),
                )
            acc_of[(j, t)] = acc

        def squares(j, t):
            acc = acc_of[(j, t)]
            ss = small.tile([P, HG], F32, name="ss")
            for h in range(HG):
                junk = small.tile([P, D], BF16, name="junk")
                nc.scalar.activation(
                    out=junk[:], in_=acc[:, h * D:(h + 1) * D], func=ACT.Square, accum_out=ss[:, h:h + 1]
                )
            ss_of[(j, t)] = ss

        def norm(j, t):
            rstd = small.tile([P, HG], F32, name="rstd")
            nc.scalar.activation(out=rstd[:], in_=ss_of[(j, t)][:], func=ACT.Abs_reciprocal_sqrt, scale=1.0 / D, bias=EPS)
            rstd_of[(j, t)] = rstd

        def products(j, t):
            acc = acc_of[(j, t)]
            tab = tabs[1] if j == KG else tabs[0]
            if t % 2 == 0:
                ab_pair = epi.tile([P, 2, 2, GROUP], F32, name="ab_pair", bufs=5)
                ab_of[(j, t // 2)] = ab_pair
            nc.vector.tensor_tensor(
                out=ab_of[(j, t // 2)][:, :, t % 2, :].rearrange("p ab (h d) -> p ab h d", d=D),
                in0=tab[:, t, :, :].unsqueeze(2).to_broadcast([P, 2, HG, D]),
                in1=acc[:].rearrange("p (h d) -> p h d", d=D).unsqueeze(1).to_broadcast([P, 2, HG, D]),
                op=ALU.mult,
            )

        def products_scaled(j, t):
            acc = acc_of[(j, t)]
            rstd = rstd_of[(j, t)]
            if t % 2 == 0:
                ab_pair = epi.tile([P, 2, 2, GROUP], F32, name="ab_pair", bufs=5)
                ab_of[(j, t // 2)] = ab_pair
            for h in range(HG):
                hs = slice(h * D, (h + 1) * D)
                nc.vector.scalar_tensor_tensor(
                    out=ab_of[(j, t // 2)][:, :, t % 2, hs],
                    in0=acc[:, hs].unsqueeze(1).to_broadcast([P, 2, D]),
                    scalar=rstd[:, h:h + 1],
                    in1=tabs[0][:, t, :, :],
                    op0=ALU.mult,
                    op1=ALU.mult,
                )

        def store_sum(j, t):
            nc.sync.dma_start(
                out=q_hbm[t * P:(t + 1) * P, j * GROUP:(j + 1) * GROUP], in_=ab_of[(j, t // 2)][:, 0, t % 2, :]
            )

        def add_pair(j, pair):
            ab_pair = ab_of[(j, pair)]
            a = ab_pair[:, 0, :, :].rearrange("p t (h two d) -> p (t h) two d", two=2, d=HALF)
            b = ab_pair[:, 1, :, :].rearrange("p t (h two d) -> p (t h) two d", two=2, d=HALF)
            nc.gpsimd.tensor_tensor(out=a, in0=a, in1=b[:, :, ::-1, :], op=ALU.add)

        def add_one(engine, j, t):
            ab_pair = ab_of[(j, t // 2)]
            a = ab_pair[:, 0, t % 2, :].rearrange("p (h two d) -> p h two d", two=2, d=HALF)
            b = ab_pair[:, 1, t % 2, :].rearrange("p (h two d) -> p h two d", two=2, d=HALF)
            engine.tensor_tensor(out=a, in0=a, in1=b[:, :, ::-1, :], op=ALU.add)

        def scale_store(j, t):
            a_sb = ab_of[(j, t // 2)][:, 0, t % 2, :]
            rstd = rstd_of[(j, t)]
            o_sb = epi.tile([P, GROUP], F32, name="o_sb", bufs=5)
            for h in range(HG):
                hs = slice(h * D, (h + 1) * D)
                nc.scalar.activation(out=o_sb[:, hs], in_=a_sb[:, hs], func=ACT.Copy, scale=rstd[:, h:h + 1])
            rows = slice(t * P, (t + 1) * P)
            if j == KG:
                nc.sync.dma_start(out=k_hbm[rows, :], in_=o_sb[:])
            else:
                nc.sync.dma_start(out=q_hbm[rows, j * GROUP:(j + 1) * GROUP], in_=o_sb[:])

        new_grouped("x")
        new_grouped(0)
        new_grouped(1)
        warm_up()
        spread_scale(0, first_cuts)
        cast(2, 0)
        spread_scale(1)
        widen_pass(0, 0, first)
        cast(2, 1)
        spread_scale(2)
        widen_pass(1, 0, whole)
        spread_scale(3)
        widen_pass(0, 1, whole)
        turn(x_sb[0], "x", 0)
        widen_pass(1, 1, whole)
        turn(x_sb[1], "x", 1)
        widen_pass(0, 2, whole)
        widen_pass(0, 3, whole)
        turn(x_sb[2], "x", 2)
        spread_weights()
        widen_pass(1, 2, whole)
        turn(x_sb[3], "x", 3)
        widen_pass(1, 3, whole)
        cast_half(2, 3)
        quant_group(0)
        quant_group("x")
        new_grouped(2)
        turn_plain(2, 0)
        turn_plain(2, 1)
        wait_for_codes("x")
        make_table(0)
        scale_half_on_gpsimd(2, 3)
        scale_out(2, 0)
        multiply(0, 0)
        multiply(0, 1)
        cast(2, 2)
        squares(0, 0)
        squares(0, 1)
        norm(0, 0)
        cast(3, 3)
        norm(0, 1)
        scale_out(2, 1)
        multiply(0, 2)
        squares(0, 2)
        multiply(0, 3)
        squares(0, 3)
        norm(0, 2)
        norm(0, 3)
        turn_plain(2, 2)
        new_grouped(KG)
        turn(wk_sb[0], KG, 0)
        turn(wk_sb[1], KG, 1)
        turn(wk_sb[2], KG, 2)
        turn(wk_sb[3], KG, 3)
        products(0, 0)
        products(0, 1)
        add_pair(0, 0)
        products(0, 2)
        products(0, 3)
        add_pair(0, 1)
        cast(3, 0)
        scale_out(2, 2)
        cast(3, 1)
        widen_other_half(2, 3)
        turn(w_scaled_of[(2, 3)], 2, 3)
        scale_store(0, 0)
        scale_store(0, 1)
        scale_store(0, 2)
        quant_group(1)
        quant_group(KG)
        wait_for_codes(KG)
        scale_on_gpsimd(3, 3)
        make_table(1)
        new_grouped(3)
        turn_plain(3, 0)
        turn_plain(3, 1)
        scale_store(0, 3)
        scale_out(3, 0)
        multiply(1, 0)
        multiply(1, 1)
        squares(1, 0)
        squares(1, 1)
        norm(1, 0)
        cast(3, 2)
        norm(1, 1)
        scale_out(3, 1)
        multiply(1, 2)
        squares(1, 2)
        multiply(1, 3)
        squares(1, 3)
        norm(1, 2)
        norm(1, 3)
        turn_plain(3, 2)
        products(1, 0)
        multiply(KG, 0)
        squares(KG, 0)
        products(1, 1)
        add_pair(1, 0)
        multiply(KG, 1)
        squares(KG, 1)
        norm(KG, 0)
        products(1, 2)
        multiply(KG, 2)
        squares(KG, 2)
        norm(KG, 1)
        products(1, 3)
        add_pair(1, 1)
        scale_store(1, 0)
        multiply(KG, 3)
        squares(KG, 3)
        norm(KG, 2)
        scale_store(1, 1)
        norm(KG, 3)
        scale_out(3, 2)
        turn(w_scaled_of[(3, 3)], 3, 3)
        scale_store(1, 2)
        scale_store(1, 3)
        products(KG, 0)
        add_one(nc.gpsimd, KG, 0)
        products(KG, 1)
        add_one(nc.gpsimd, KG, 1)
        products(KG, 2)
        products(KG, 3)
        scale_store(KG, 0)
        scale_store(KG, 1)
        quant_group(2)
        quant_group(3)
        multiply(2, 0)
        squares(2, 0)
        multiply(2, 1)
        squares(2, 1)
        norm(2, 0)
        products(2, 0)
        add_one(nc.gpsimd, 2, 0)
        add_pair(KG, 1)
        multiply(2, 2)
        squares(2, 2)
        norm(2, 1)
        products(2, 1)
        add_one(nc.gpsimd, 2, 1)
        multiply(2, 3)
        squares(2, 3)
        norm(2, 2)
        scale_store(2, 0)
        products(2, 2)
        add_one(nc.gpsimd, 2, 2)
        norm(2, 3)
        multiply(3, 0)
        squares(3, 0)
        products(2, 3)
        add_one(nc.gpsimd, 2, 3)
        multiply(3, 1)
        norm(3, 0)
        squares(3, 1)
        multiply(3, 2)
        norm(3, 1)
        products_scaled(3, 0)
        squares(3, 2)
        multiply(3, 3)
        norm(3, 2)
        products_scaled(3, 1)
        squares(3, 3)
        scale_store(KG, 2)
        norm(3, 3)
        scale_store(KG, 3)
        products_scaled(3, 2)
        scale_store(2, 1)
        products_scaled(3, 3)
        scale_store(2, 2)
        add_one(nc.vector, 3, 0)
        store_sum(3, 0)
        scale_store(2, 3)
        add_one(nc.vector, 3, 1)
        store_sum(3, 1)
        add_one(nc.vector, 3, 2)
        store_sum(3, 2)
        add_one(nc.vector, 3, 3)
        store_sum(3, 3)
